import numpy as np
import ml_dtypes


def mxq(x, axis, fmt="e4m3"):
    dtype, down = {"e4m3": (ml_dtypes.float8_e4m3fn, 7), "e5m2": (ml_dtypes.float8_e5m2, 14)}[fmt]
    v = np.moveaxis(np.asarray(x, np.float32).astype(ml_dtypes.bfloat16).astype(np.float64), axis, -1)
    blocks = v.reshape(v.shape[:-1] + (-1, 32))
    amax = np.abs(blocks).max(-1, keepdims=True)
    byte = np.maximum(np.where(amax > 0, np.frexp(amax)[1] - 1 + 127, 0) - down, 1)
    scale = np.exp2(byte - 127.0)
    codes = (blocks / scale).astype(np.float32).astype(dtype).astype(np.float64)
    return np.moveaxis((codes * scale).reshape(v.shape), -1, axis)


WIDE = False


def mx_kscale(k):
    if not WIDE:
        return np.ones(k)
    levels = np.array([10, -10, 5, -5, 0])
    a = np.random.permutation(np.resize(levels, k // 512 * 4)).reshape(k // 512, 4)
    idx = np.arange(k)
    return np.exp2(a[idx // 512, idx % 128 // 32])


BF16 = ml_dtypes.bfloat16


def bf(x):
    return np.asarray(x, np.float32).astype(BF16)


def f64(x):
    return np.asarray(x).astype(np.float64)


E2M1 = np.array([0.0, 0.5, 1.0, 1.5, 2.0, 3.0, 4.0, 6.0, -0.0, -0.5, -1.0, -1.5, -2.0, -3.0, -4.0, -6.0])


def pack_weight(w, fmt):
    k, n = w.shape
    w = f64(bf(w)).reshape(k // 32, 32, n)
    amax = np.abs(w).max(1)
    if fmt == "e4m3":
        byte = np.frexp(amax)[1] - 1 + 127 - 7
    else:
        mant, ex = np.frexp(amax / 6.0)
        byte = np.where(mant > 0.5, ex, ex - 1) + 127
    byte = np.clip(np.where(amax > 0, byte, 1), 1, 254)
    scaled = (w * np.exp2(127.0 - byte)[:, None, :]).reshape(k, n).astype(np.float32)
    by_word = np.ascontiguousarray(scaled.reshape(k // 512, 128, 4, n).transpose(0, 1, 3, 2))
    if fmt == "e4m3":
        words = by_word.astype(ml_dtypes.float8_e4m3fn).view(np.uint8)
    else:
        c = by_word.astype(ml_dtypes.float4_e2m1fn).view(np.uint8) & 0xF
        words = c[..., 0::2] | (c[..., 1::2] << 4)
    return np.ascontiguousarray(words), np.ascontiguousarray(byte.astype(np.uint8).reshape(k // 512, 16, n))


def unpack_weight(words, scales, fmt):
    g, p, n, _ = words.shape
    if fmt == "e4m3":
        vals = np.ascontiguousarray(words).view(ml_dtypes.float8_e4m3fn).astype(np.float64)
    else:
        nib = np.empty((g, p, n, 4), np.uint8)
        nib[..., 0::2] = words & 0xF
        nib[..., 1::2] = words >> 4
        vals = E2M1[nib]
    vals = vals * np.repeat(np.exp2(scales.astype(np.float64) - 127.0), 8, axis=1)[..., None]
    return vals.transpose(0, 1, 3, 2).reshape(g * 512, n)

def pack4(w):
    words, scales = pack_weight(w, "e2m1")
    return words.reshape(words.shape[0], 128, -1), scales


def unpack4(words, scales):
    return unpack_weight(words.reshape(words.shape[0], 128, -1, 2), scales, "e2m1")


T, B, I, H = 32, 128, 512, 512


def sigmoid(v):
    return 1.0 / (1.0 + np.exp(-v))


def setup_inputs():
    s = mx_kscale(I)
    inp = bf(np.random.standard_normal((T, B, I)) * s)
    h0 = bf(np.random.standard_normal((B, H)))
    c0 = bf(np.random.standard_normal((B, H)))
    noise = bf(np.random.standard_normal((B, H)) * 0.3)
    w_ih = np.random.standard_normal((4 * H, I)) / np.sqrt(I) / s[None, :]
    words, scales = pack4(np.ascontiguousarray(w_ih.T))
    return {
        "input": inp,
        "h0": h0,
        "c0": c0,
        "noise": noise,
        "W_ih_words": words,
        "W_ih_scales": scales,
        "W_hh": bf(np.random.standard_normal((4 * H, H)) * 0.7 / np.sqrt(H)),
        "b_ih": bf(np.random.standard_normal(4 * H) * 0.3),
        "b_hh": bf(np.random.standard_normal(4 * H) * 0.3),
    }


def reference(input, h0, c0, noise, W_ih_words, W_ih_scales, W_hh, b_ih, b_hh):
    hsz = h0.shape[-1]
    gx = mxq(f64(input), 2, "e4m3") @ unpack4(W_ih_words, W_ih_scales)
    gh = f64(h0) @ f64(W_hh).T
    gates = gx + gh[None, :, :] + (f64(b_ih) + f64(b_hh))
    i_g = sigmoid(gates[..., 0 * hsz:1 * hsz])
    f_g = sigmoid(gates[..., 1 * hsz:2 * hsz])
    g_g = np.tanh(gates[..., 2 * hsz:3 * hsz])
    o_g = sigmoid(gates[..., 3 * hsz:4 * hsz])
    c = f_g * f64(c0)[None] + i_g * g_g
    h = o_g * np.tanh(c) + f64(noise)[None]
    return (h, np.stack([h[-1], c[-1]]))

@@ -1,0 +1,294 @@
+from contextlib import ExitStack
+
+import concourse.mybir as mybir
+from concourse.masks import make_identity
+
+F32 = mybir.dt.float32
+BF16 = mybir.dt.bfloat16
+I32 = mybir.dt.int32
+U8 = mybir.dt.uint8
+U32 = mybir.dt.uint32
+FP8X4 = mybir.dt.float8_e4m3fn_x4
+FP4X4 = mybir.dt.float4_e2m1fn_x4
+ACT = mybir.ActivationFunctionType
+ALU = mybir.AluOpType
+
+P = 128
+STEPS = 32
+K = 512
+H = 512
+GATES = 4
+GATE_I, GATE_F, GATE_G, GATE_O = 0, 1, 2, 3
+WORDS = K // 2
+STEPS_PER_LOAD = 4
+STEPS_PER_BANK = 2
+STEPS_PER_GROUP = 2
+GROUPS = STEPS // STEPS_PER_GROUP
+LOADS = STEPS // STEPS_PER_LOAD
+GROUPS_PER_LOAD = STEPS_PER_LOAD // STEPS_PER_GROUP
+GATE_ORDER = (GATE_I, GATE_G, GATE_F, GATE_O)
+GROUPS_WITHOUT_HELPER = 1
+WARM_UP = 6
+
+FLOPS = 2 * STEPS * P * K * GATES * H + 2 * P * H * GATES * H
+
+
+def tile_lstmlayer_kernel(
+    tc, x, h0, c0, noise, w_ih_words, w_ih_scales, w_hh, b_ih, b_hh, out_h, out_state
+):
+    nc = tc.nc
+    with ExitStack() as ctx:
+        ctx.enter_context(tc.manual_schedule())
+        keep = ctx.enter_context(tc.tile_pool(name="keep", bufs=1))
+        stage = ctx.enter_context(tc.tile_pool(name="stage", bufs=2))
+        work = ctx.enter_context(tc.tile_pool(name="work", bufs=2))
+        fixed_psum = ctx.enter_context(tc.psum_pool(name="fixed_psum", bufs=1))
+        psum = ctx.enter_context(tc.psum_pool(name="psum", bufs=6))
+
+        ident_f32 = keep.tile([P, P], F32)
+        make_identity(nc, ident_f32[:])
+        ident_bf16 = keep.tile([P, P], BF16)
+        make_identity(nc, ident_bf16[:])
+        ones = keep.tile([P, P], BF16)
+        nc.gpsimd.memset(ones[:], 1.0)
+
+        warm = keep.tile([P, 1], F32)
+        nc.vector.memset(warm[:], 0.0)
+        nc.scalar.activation(out=warm[:], in_=warm[:], func=ACT.Sigmoid)
+
+        bias_rows = keep.tile([P, GATES * H], BF16)
+        nc.vector.memset(bias_rows[:].bitcast(I32), 0)
+        w_scale_plane = keep.tile([P, GATES * H], U8, align_bytes=64)
+        nc.vector.memset(w_scale_plane[:].bitcast(I32), 0)
+
+        warm_ps = psum.tile([P, H], F32, tag="bank", name="warm_ps")
+        for k in range(WARM_UP):
+            nc.tensor.matmul(out=warm_ps[:, 0:P], lhsT=ident_f32[:], rhs=ident_f32[:], start=True, stop=True)
+
+        x_codes = keep.tile([P, STEPS, P], U32, align_bytes=64)
+        x_scales = keep.tile([P, STEPS, P], U8, align_bytes=64)
+        x_loads = []
+        grouped_tiles = {}
+
+        def load_x(c):
+            x_sb = keep.tile([P, STEPS_PER_LOAD, K], BF16, name="x_sb%d" % c)
+            nc.sync.dma_start(
+                out=x_sb[:],
+                in_=x[STEPS_PER_LOAD * c : STEPS_PER_LOAD * (c + 1)].rearrange("t b k -> b t k"),
+            )
+            x_loads.append(x_sb)
+
+        def regroup_x(c):
+            x_words = x_loads[c][:].rearrange("b s k -> b (s k)").bitcast(F32)
+            grouped = stage.tile([P, STEPS_PER_LOAD * P * 4], BF16, align_bytes=64, name="grouped")
+            grouped_tiles[c] = grouped
+            grouped_words = grouped[:].bitcast(F32).rearrange(
+                "p (s b u) -> p s b u", s=STEPS_PER_LOAD, u=2
+            )
+            for q in range(STEPS_PER_LOAD // STEPS_PER_BANK):
+                x_t_ps = psum.tile([P, STEPS_PER_BANK, 2, P], F32, tag="bank", name="x_t_ps")
+                for s in range(STEPS_PER_BANK):
+                    first = WORDS * (STEPS_PER_BANK * q + s)
+                    for u in range(2):
+                        nc.tensor.transpose(
+                            x_t_ps[:, s, u, :], x_words[:, first + u : first + WORDS : 2], ident_f32[:]
+                        )
+                nc.scalar.copy(
+                    out=grouped_words[:, STEPS_PER_BANK * q : STEPS_PER_BANK * (q + 1)],
+                    in_=x_t_ps[:].rearrange("p s u b -> p s b u"),
+                )
+
+        def quantise_x(c):
+            steps = slice(STEPS_PER_LOAD * c, STEPS_PER_LOAD * (c + 1))
+            nc.vector.quantize_mx(
+                out=x_codes[:, steps, :].rearrange("p s b -> p (s b)").bitcast(FP8X4),
+                scales=x_scales[:, steps, :].rearrange("p s b -> p (s b)"),
+                in_=grouped_tiles[c][:],
+            )
+
+        const = keep.tile([P, GATES, H], F32)
+        w_words = keep.tile([P, 2 * GATES * H], U8, align_bytes=64)
+        c0_sb = keep.tile([P, H], BF16)
+        noise_sb = keep.tile([P, H], BF16)
+        h0_sb = keep.tile([P, H], BF16)
+        whh_sb = keep.tile([P, GATES, 4, H], BF16)
+
+        def load_whh(j):
+            nc.sync.dma_start(
+                out=whh_sb[:, j],
+                in_=w_hh[H * j : H * (j + 1), :].rearrange("(p a) k -> p a k", a=4),
+            )
+
+        nc.sync.dma_start(out=h0_sb[:], in_=h0)
+        load_whh(GATE_ORDER[0])
+        load_x(0)
+        load_whh(GATE_ORDER[1])
+        nc.sync.dma_start(out=w_words[:].bitcast(I32), in_=w_ih_words[0].bitcast(I32))
+        nc.sync.dma_start(out=bias_rows[0:1, :], in_=b_ih.rearrange("(o n) -> o n", o=1))
+        nc.sync.dma_start(out=bias_rows[1:2, :], in_=b_hh.rearrange("(o n) -> o n", o=1))
+        for quad in range(4):
+            nc.sync.dma_start(
+                out=w_scale_plane[32 * quad : 32 * quad + 4, :].bitcast(I32),
+                in_=w_ih_scales[0, 4 * quad : 4 * quad + 4, :].bitcast(I32),
+            )
+        for j in GATE_ORDER[2:]:
+            load_whh(j)
+        nc.sync.dma_start(out=c0_sb[:], in_=c0)
+        nc.sync.dma_start(out=noise_sb[:], in_=noise)
+        for c in range(1, LOADS):
+            load_x(c)
+
+        h0_t_ps = psum.tile([P, 2, P], F32, tag="bank")
+        for half in range(2):
+            nc.tensor.transpose(
+                h0_t_ps[:, half, :], h0_sb[:].bitcast(F32)[:, P * half : P * (half + 1)], ident_f32[:]
+            )
+        h0_t = keep.tile([P, 2, P], F32)
+        nc.vector.tensor_copy(out=h0_t[:], in_=h0_t_ps[:])
+        h0_rows = keep.tile([P, 2, 2, P], BF16)
+        nc.vector.tensor_copy(
+            out=h0_rows[:], in_=h0_t[:].bitcast(BF16).rearrange("w half (b e) -> w half e b", e=2)
+        )
+        whh_t = keep.tile([P, 2, GATES * H], F32)
+
+        def transpose_whh(j):
+            for half in range(2):
+                whh_t_ps = psum.tile([P, 4, P], F32, tag="bank", name="whh_t_ps")
+                for a in range(4):
+                    nc.tensor.transpose(
+                        whh_t_ps[:, a, :],
+                        whh_sb[:, j, a, :].bitcast(F32)[:, P * half : P * (half + 1)],
+                        ident_f32[:],
+                    )
+                dst = whh_t[:, half, H * j : H * (j + 1)].rearrange("w (p a) -> w p a", a=4)
+                src = whh_t_ps[:].rearrange("w a p -> w p a")
+                if half == 0:
+                    nc.vector.tensor_copy(out=dst, in_=src)
+                else:
+                    nc.scalar.copy(out=dst, in_=src)
+
+        def make_const(j):
+            const_ps = psum.tile([P, H], F32, tag="bank", name="const_ps")
+            for half in range(2):
+                for e in range(2):
+                    nc.tensor.matmul(
+                        out=const_ps[:],
+                        lhsT=h0_rows[:, half, e, :],
+                        rhs=whh_t[:, half, H * j : H * (j + 1)]
+                        .bitcast(BF16)
+                        .rearrange("w (n e) -> w n e", e=2)[:, :, e],
+                        start=(half == 0 and e == 0),
+                        stop=False,
+                    )
+            nc.tensor.matmul(
+                out=const_ps[:], lhsT=ones[:], rhs=bias_rows[:, H * j : H * (j + 1)], start=False, stop=True
+            )
+            nc.vector.tensor_copy(out=const[:, j, :], in_=const_ps[:])
+
+        transpose_whh(GATE_ORDER[0])
+        regroup_x(0)
+        transpose_whh(GATE_ORDER[1])
+        quantise_x(0)
+
+        c0_ps = fixed_psum.tile([P, H], F32)
+        noise_ps = fixed_psum.tile([P, H], F32)
+
+        def fix_in_psum():
+            nc.tensor.matmul(out=c0_ps[:], lhsT=ident_bf16[:], rhs=c0_sb[:], start=True, stop=True)
+            nc.tensor.matmul(out=noise_ps[:], lhsT=ident_bf16[:], rhs=noise_sb[:], start=True, stop=True)
+
+        group_shape = [P, STEPS_PER_GROUP, H]
+        c0_bc = c0_ps[:].unsqueeze(1).to_broadcast(group_shape)
+        noise_bc = noise_ps[:].unsqueeze(1).to_broadcast(group_shape)
+        gates, cell, o_tanh_c = {}, {}, {}
+
+        def project(n, gate):
+            if n == 0:
+                make_const(gate)
+            for s in range(STEPS_PER_GROUP):
+                t = STEPS_PER_GROUP * n + s
+                gate_ps = psum.tile([P, H], F32, tag="bank", name="gate_ps")
+                nc.tensor.matmul_mx(
+                    out=gate_ps[:],
+                    lhsT=x_codes[:, t, :].bitcast(FP8X4),
+                    lhsT_scale=x_scales[:, t, :],
+                    rhs=w_words[:, 2 * H * gate : 2 * H * (gate + 1)].bitcast(FP4X4),
+                    rhs_scale=w_scale_plane[:, H * gate : H * (gate + 1)],
+                    start=True,
+                    stop=True,
+                )
+                nc.vector.tensor_tensor(
+                    out=gates[n][:, gate, s, :], in0=gate_ps[:], in1=const[:, gate, :], op=ALU.add
+                )
+            nc.scalar.activation(
+                out=gates[n][:, gate],
+                in_=gates[n][:, gate],
+                func=(ACT.Tanh if gate == GATE_G else ACT.Sigmoid),
+            )
+            place = GATE_ORDER.index(gate)
+            if n == 0 and place + 2 < GATES:
+                transpose_whh(GATE_ORDER[place + 2])
+
+        def helper(n):
+            return nc.vector if n >= GROUPS - GROUPS_WITHOUT_HELPER else nc.gpsimd
+
+        def pieces(n):
+            if n < GROUPS - 1:
+                return [slice(0, STEPS_PER_GROUP)]
+            return [slice(s, s + 1) for s in range(STEPS_PER_GROUP)]
+
+        def store_h(n):
+            h = work.tile(group_shape, F32, name="h")
+            for steps in pieces(n):
+                nc.vector.tensor_tensor(
+                    out=h[:, steps], in0=o_tanh_c[n][:, steps], in1=noise_bc[:, steps], op=ALU.add
+                )
+                first = STEPS_PER_GROUP * n
+                nc.sync.dma_start(
+                    out=out_h[first + steps.start : first + steps.stop].rearrange("t b m -> b t m"),
+                    in_=h[:, steps],
+                )
+            if n == GROUPS - 1:
+                nc.scalar.dma_start(out=out_state[0], in_=h[:, STEPS_PER_GROUP - 1, :])
+
+        for n in range(GROUPS + 2):
+            next_load = n // GROUPS_PER_LOAD + 1
+            if n < GROUPS:
+                gates[n] = work.tile([P, GATES, STEPS_PER_GROUP, H], F32, bufs=4, name="gates")
+                project(n, GATE_I)
+                project(n, GATE_G)
+                i_g = work.tile(group_shape, F32, name="i_g")
+                nc.gpsimd.tensor_tensor(
+                    out=i_g[:], in0=gates[n][:, GATE_I], in1=gates[n][:, GATE_G], op=ALU.mult
+                )
+                project(n, GATE_F)
+            if n >= 2:
+                store_h(n - 2)
+            if 1 <= n <= GROUPS:
+                tanh_c = work.tile(group_shape, F32, name="tanh_c")
+                o_tanh_c[n - 1] = work.tile(group_shape, F32, name="o_tanh_c")
+                for steps in pieces(n - 1):
+                    nc.scalar.activation(out=tanh_c[:, steps], in_=cell[n - 1][:, steps], func=ACT.Tanh)
+                for steps in pieces(n - 1):
+                    helper(n - 1).tensor_tensor(
+                        out=o_tanh_c[n - 1][:, steps],
+                        in0=gates[n - 1][:, GATE_O, steps],
+                        in1=tanh_c[:, steps],
+                        op=ALU.mult,
+                    )
+            if n < GROUPS:
+                project(n, GATE_O)
+                if n % GROUPS_PER_LOAD == 1 and next_load < LOADS:
+                    quantise_x(next_load)
+            if n == 0:
+                fix_in_psum()
+            if n < GROUPS:
+                f_c0 = work.tile(group_shape, F32, name="f_c0")
+                nc.vector.tensor_tensor(out=f_c0[:], in0=gates[n][:, GATE_F], in1=c0_bc, op=ALU.mult)
+                cell[n] = work.tile(group_shape, F32, name="cell")
+                for steps in pieces(n):
+                    helper(n).tensor_tensor(out=cell[n][:, steps], in0=f_c0[:, steps], in1=i_g[:, steps], op=ALU.add)
+                if n == GROUPS - 1:
+                    nc.scalar.dma_start(out=out_state[1], in_=cell[n][:, STEPS_PER_GROUP - 1, :])
+            if n % GROUPS_PER_LOAD == 0 and next_load < LOADS:
+                regroup_x(next_load)

@@ -27,7 +27,10 @@ GROUPS = STEPS // STEPS_PER_GROUP
 LOADS = STEPS // STEPS_PER_LOAD
 GROUPS_PER_LOAD = STEPS_PER_LOAD // STEPS_PER_GROUP
 GATE_ORDER = (GATE_I, GATE_G, GATE_F, GATE_O)
+BLOCKS_ON_VECTOR = 2
 GROUPS_WITHOUT_HELPER = 1
+BLOCKS = H // P
+BLOCKS_PER_BANK = 2
 WARM_UP = 6
 
 FLOPS = 2 * STEPS * P * K * GATES * H + 2 * P * H * GATES * H
@@ -43,7 +46,8 @@ def tile_lstmlayer_kernel(
         stage = ctx.enter_context(tc.tile_pool(name="stage", bufs=2))
         work = ctx.enter_context(tc.tile_pool(name="work", bufs=2))
         fixed_psum = ctx.enter_context(tc.psum_pool(name="fixed_psum", bufs=1))
-        psum = ctx.enter_context(tc.psum_pool(name="psum", bufs=6))
+        psum = ctx.enter_context(tc.psum_pool(name="psum", bufs=4))
+        cell_psum = ctx.enter_context(tc.psum_pool(name="cell_psum", bufs=2))
 
         ident_f32 = keep.tile([P, P], F32)
         make_identity(nc, ident_f32[:])
@@ -78,25 +82,25 @@ def tile_lstmlayer_kernel(
             )
             x_loads.append(x_sb)
 
-        def regroup_x(c):
+        x_t = {}
+
+        def turn_x(c, q):
             x_words = x_loads[c][:].rearrange("b s k -> b (s k)").bitcast(F32)
-            grouped = stage.tile([P, STEPS_PER_LOAD * P * 4], BF16, align_bytes=64, name="grouped")
-            grouped_tiles[c] = grouped
-            grouped_words = grouped[:].bitcast(F32).rearrange(
-                "p (s b u) -> p s b u", s=STEPS_PER_LOAD, u=2
+            x_t_ps = psum.tile([P, STEPS_PER_BANK, 2, P], F32, tag="bank", name="x_t_ps")
+            for s in range(STEPS_PER_BANK):
+                first = WORDS * (STEPS_PER_BANK * q + s)
+                for u in range(2):
+                    nc.tensor.transpose(x_t_ps[:, s, u, :], x_words[:, first + u : first + WORDS : 2], ident_f32[:])
+            x_t[c, q] = x_t_ps
+
+        def copy_x(c, q):
+            if q == 0:
+                grouped_tiles[c] = stage.tile([P, STEPS_PER_LOAD * P * 4], BF16, align_bytes=64, name="grouped")
+            grouped_words = grouped_tiles[c][:].bitcast(F32).rearrange("p (s b u) -> p s b u", s=STEPS_PER_LOAD, u=2)
+            nc.scalar.copy(
+                out=grouped_words[:, STEPS_PER_BANK * q : STEPS_PER_BANK * (q + 1)],
+                in_=x_t[c, q][:].rearrange("p s u b -> p s b u"),
             )
-            for q in range(STEPS_PER_LOAD // STEPS_PER_BANK):
-                x_t_ps = psum.tile([P, STEPS_PER_BANK, 2, P], F32, tag="bank", name="x_t_ps")
-                for s in range(STEPS_PER_BANK):
-                    first = WORDS * (STEPS_PER_BANK * q + s)
-                    for u in range(2):
-                        nc.tensor.transpose(
-                            x_t_ps[:, s, u, :], x_words[:, first + u : first + WORDS : 2], ident_f32[:]
-                        )
-                nc.scalar.copy(
-                    out=grouped_words[:, STEPS_PER_BANK * q : STEPS_PER_BANK * (q + 1)],
-                    in_=x_t_ps[:].rearrange("p s u b -> p s b u"),
-                )
 
         def quantise_x(c):
             steps = slice(STEPS_PER_LOAD * c, STEPS_PER_LOAD * (c + 1))
@@ -106,7 +110,8 @@ def tile_lstmlayer_kernel(
                 in_=grouped_tiles[c][:],
             )
 
-        const = keep.tile([P, GATES, H], F32)
+        const_o = keep.tile([P, H], F32)
+        const_t = keep.tile([P, GATES, BLOCKS, P], F32)
         w_words = keep.tile([P, 2 * GATES * H], U8, align_bytes=64)
         c0_sb = keep.tile([P, H], BF16)
         noise_sb = keep.tile([P, H], BF16)
@@ -151,9 +156,9 @@ def tile_lstmlayer_kernel(
         )
         whh_t = keep.tile([P, 2, GATES * H], F32)
 
-        def transpose_whh(j):
+        def transpose_whh(j, engines):
             for half in range(2):
-                whh_t_ps = psum.tile([P, 4, P], F32, tag="bank", name="whh_t_ps")
+                whh_t_ps = cell_psum.tile([P, 4, P], F32, tag="cell", name="whh_t_ps")
                 for a in range(4):
                     nc.tensor.transpose(
                         whh_t_ps[:, a, :],
@@ -162,13 +167,30 @@ def tile_lstmlayer_kernel(
                     )
                 dst = whh_t[:, half, H * j : H * (j + 1)].rearrange("w (p a) -> w p a", a=4)
                 src = whh_t_ps[:].rearrange("w a p -> w p a")
-                if half == 0:
+                if engines[half] == "v":
                     nc.vector.tensor_copy(out=dst, in_=src)
                 else:
                     nc.scalar.copy(out=dst, in_=src)
 
         def make_const(j):
             const_ps = psum.tile([P, H], F32, tag="bank", name="const_ps")
+            if j != GATE_O:
+                for blk in range(BLOCKS):
+                    cols = slice(H * j + P * blk, H * j + P * (blk + 1))
+                    for half in range(2):
+                        for e in range(2):
+                            nc.tensor.matmul(
+                                out=const_ps[:, P * blk : P * (blk + 1)],
+                                lhsT=whh_t[:, half, cols].bitcast(BF16).rearrange("w (n e) -> w n e", e=2)[:, :, e],
+                                rhs=h0_rows[:, half, e, :],
+                                start=(half == 0 and e == 0),
+                                stop=False,
+                            )
+                    nc.tensor.matmul(
+                        out=const_ps[:, P * blk : P * (blk + 1)], lhsT=bias_rows[:, cols], rhs=ones[:], start=False, stop=True
+                    )
+                nc.vector.tensor_copy(out=const_t[:, j].rearrange("p k b -> p (k b)"), in_=const_ps[:])
+                return
             for half in range(2):
                 for e in range(2):
                     nc.tensor.matmul(
@@ -183,51 +205,82 @@ def tile_lstmlayer_kernel(
             nc.tensor.matmul(
                 out=const_ps[:], lhsT=ones[:], rhs=bias_rows[:, H * j : H * (j + 1)], start=False, stop=True
             )
-            nc.vector.tensor_copy(out=const[:, j, :], in_=const_ps[:])
+            nc.vector.tensor_copy(out=const_o[:], in_=const_ps[:])
 
-        transpose_whh(GATE_ORDER[0])
-        regroup_x(0)
-        transpose_whh(GATE_ORDER[1])
-        quantise_x(0)
 
-        c0_ps = fixed_psum.tile([P, H], F32)
+        c0_ps = fixed_psum.tile([P, BLOCKS, P], F32)
+        c0_t = keep.tile([P, BLOCKS - BLOCKS_ON_VECTOR, P], F32)
         noise_ps = fixed_psum.tile([P, H], F32)
 
         def fix_in_psum():
-            nc.tensor.matmul(out=c0_ps[:], lhsT=ident_bf16[:], rhs=c0_sb[:], start=True, stop=True)
+            for blk in range(BLOCKS):
+                nc.tensor.matmul(
+                    out=c0_ps[:, blk, :], lhsT=c0_sb[:, P * blk : P * (blk + 1)], rhs=ident_bf16[:], start=True, stop=True
+                )
+            nc.scalar.copy(out=c0_t[:], in_=c0_ps[:, BLOCKS_ON_VECTOR:BLOCKS, :])
             nc.tensor.matmul(out=noise_ps[:], lhsT=ident_bf16[:], rhs=noise_sb[:], start=True, stop=True)
 
         group_shape = [P, STEPS_PER_GROUP, H]
-        c0_bc = c0_ps[:].unsqueeze(1).to_broadcast(group_shape)
+        turned = "p (k s b) -> p k s b"
         noise_bc = noise_ps[:].unsqueeze(1).to_broadcast(group_shape)
-        gates, cell, o_tanh_c = {}, {}, {}
+        gates, i_gs, f_c0s, cell, o_tanh_c = {}, {}, {}, {}, {}
 
-        def project(n, gate):
-            if n == 0:
-                make_const(gate)
-            for s in range(STEPS_PER_GROUP):
-                t = STEPS_PER_GROUP * n + s
-                gate_ps = psum.tile([P, H], F32, tag="bank", name="gate_ps")
-                nc.tensor.matmul_mx(
-                    out=gate_ps[:],
-                    lhsT=x_codes[:, t, :].bitcast(FP8X4),
-                    lhsT_scale=x_scales[:, t, :],
-                    rhs=w_words[:, 2 * H * gate : 2 * H * (gate + 1)].bitcast(FP4X4),
-                    rhs_scale=w_scale_plane[:, H * gate : H * (gate + 1)],
-                    start=True,
-                    stop=True,
-                )
-                nc.vector.tensor_tensor(
-                    out=gates[n][:, gate, s, :], in0=gate_ps[:], in1=const[:, gate, :], op=ALU.add
-                )
+        def turned_view(tile_2d):
+            return tile_2d.rearrange(turned, k=BLOCKS, s=STEPS_PER_GROUP)
+
+        banks = {}
+
+        def multiply(n, gate):
+            first = STEPS_PER_GROUP * n
+            for bank in range(2):
+                if gate == GATE_O:
+                    gate_ps = psum.tile([P, H], F32, tag="bank", name="gate_ps")
+                    nc.tensor.matmul_mx(
+                        out=gate_ps[:],
+                        lhsT=x_codes[:, first + bank, :].bitcast(FP8X4),
+                        lhsT_scale=x_scales[:, first + bank, :],
+                        rhs=w_words[:, 2 * H * gate : 2 * H * (gate + 1)].bitcast(FP4X4),
+                        rhs_scale=w_scale_plane[:, H * gate : H * (gate + 1)],
+                        start=True,
+                        stop=True,
+                    )
+                else:
+                    gate_ps = psum.tile([P, BLOCKS_PER_BANK, STEPS_PER_GROUP, P], F32, tag="bank", name="gate_ps")
+                    for k in range(BLOCKS_PER_BANK):
+                        col = H * gate + P * (BLOCKS_PER_BANK * bank + k)
+                        nc.tensor.matmul_mx(
+                            out=gate_ps[:, k].rearrange("p s b -> p (s b)"),
+                            lhsT=w_words[:, 2 * col : 2 * (col + P)].bitcast(FP4X4),
+                            lhsT_scale=w_scale_plane[:, col : col + P],
+                            rhs=x_codes[:, first : first + STEPS_PER_GROUP, :].rearrange("p s b -> p (s b)").bitcast(FP8X4),
+                            rhs_scale=x_scales[:, first : first + STEPS_PER_GROUP, :].rearrange("p s b -> p (s b)"),
+                            start=True,
+                            stop=True,
+                        )
+                banks[n, gate, bank] = gate_ps
+
+        def add_const(n, gate):
+            for bank in range(2):
+                gate_ps = banks[n, gate, bank]
+                if gate == GATE_O:
+                    nc.vector.tensor_tensor(
+                        out=gates[n][:, gate, H * bank : H * (bank + 1)], in0=gate_ps[:], in1=const_o[:], op=ALU.add
+                    )
+                else:
+                    blocks = slice(BLOCKS_PER_BANK * bank, BLOCKS_PER_BANK * (bank + 1))
+                    nc.vector.tensor_tensor(
+                        out=turned_view(gates[n][:, gate])[:, blocks],
+                        in0=gate_ps[:],
+                        in1=const_t[:, gate, blocks, :].unsqueeze(2).to_broadcast([P, BLOCKS_PER_BANK, STEPS_PER_GROUP, P]),
+                        op=ALU.add,
+                    )
+
+        def activate(n, gate):
             nc.scalar.activation(
                 out=gates[n][:, gate],
                 in_=gates[n][:, gate],
                 func=(ACT.Tanh if gate == GATE_G else ACT.Sigmoid),
             )
-            place = GATE_ORDER.index(gate)
-            if n == 0 and place + 2 < GATES:
-                transpose_whh(GATE_ORDER[place + 2])
 
         def helper(n):
             return nc.vector if n >= GROUPS - GROUPS_WITHOUT_HELPER else nc.gpsimd
@@ -251,44 +304,138 @@ def tile_lstmlayer_kernel(
             if n == GROUPS - 1:
                 nc.scalar.dma_start(out=out_state[0], in_=h[:, STEPS_PER_GROUP - 1, :])
 
-        for n in range(GROUPS + 2):
-            next_load = n // GROUPS_PER_LOAD + 1
-            if n < GROUPS:
-                gates[n] = work.tile([P, GATES, STEPS_PER_GROUP, H], F32, bufs=4, name="gates")
-                project(n, GATE_I)
-                project(n, GATE_G)
-                i_g = work.tile(group_shape, F32, name="i_g")
-                nc.gpsimd.tensor_tensor(
-                    out=i_g[:], in0=gates[n][:, GATE_I], in1=gates[n][:, GATE_G], op=ALU.mult
+        def sum_cell(n, s):
+            c_ps = cell_psum.tile([P, BLOCKS, P], F32, tag="cell", name="c_ps")
+            for k, product in enumerate((i_gs[n], f_c0s[n])):
+                for blk in range(BLOCKS):
+                    nc.tensor.matmul(
+                        out=c_ps[:, blk, :],
+                        lhsT=product[:, blk, s, :],
+                        rhs=ident_f32[:],
+                        is_transpose=True,
+                        start=(k == 0 and blk == 0),
+                        stop=(k == 1 and blk == BLOCKS - 1),
+                    )
+            cell[n, s] = c_ps
+
+        def tanh_cell(n, s):
+            nc.scalar.activation(
+                out=tanh_c[n][:, s], in_=cell[n, s][:].rearrange("p k b -> p (k b)"), func=ACT.Tanh
+            )
+            if n == GROUPS - 1 and s == STEPS_PER_GROUP - 1:
+                c_last = keep.tile([P, H], F32)
+                nc.scalar.copy(out=c_last[:], in_=cell[n, s][:].rearrange("p k b -> p (k b)"))
+                nc.scalar.dma_start(out=out_state[1], in_=c_last[:])
+
+        turned_shape = [P, BLOCKS, STEPS_PER_GROUP, P]
+        tanh_c = {}
+
+        def mul_i_g(n):
+            i_gs[n] = work.tile(turned_shape, F32, name="i_g")
+            nc.gpsimd.tensor_tensor(
+                out=i_gs[n][:],
+                in0=turned_view(gates[n][:, GATE_I]),
+                in1=turned_view(gates[n][:, GATE_G]),
+                op=ALU.mult,
+            )
+
+        def mul_f_c0(n, engine):
+            if n not in f_c0s:
+                f_c0s[n] = work.tile(turned_shape, F32, name="f_c0")
+            mine = slice(0, BLOCKS_ON_VECTOR) if engine == nc.vector else slice(BLOCKS_ON_VECTOR, BLOCKS)
+            count = mine.stop - mine.start
+            source = c0_ps[:, mine, :] if engine == nc.vector else c0_t[:]
+            engine.tensor_tensor(
+                out=f_c0s[n][:, mine],
+                in0=turned_view(gates[n][:, GATE_F])[:, mine],
+                in1=source.unsqueeze(2).to_broadcast([P, count, STEPS_PER_GROUP, P]),
+                op=ALU.mult,
+            )
+
+        def mul_o(n):
+            o_tanh_c[n] = work.tile(group_shape, F32, name="o_tanh_c")
+            for steps in pieces(n):
+                helper(n).tensor_tensor(
+                    out=o_tanh_c[n][:, steps],
+                    in0=gates[n][:, GATE_O].rearrange("p (s m) -> p s m", s=STEPS_PER_GROUP)[:, steps],
+                    in1=tanh_c[n][:, steps],
+                    op=ALU.mult,
                 )
-                project(n, GATE_F)
+
+        def start_group(n):
+            gates[n] = work.tile([P, GATES, STEPS_PER_GROUP * H], F32, bufs=4, name="gates")
+
+        transpose_whh(GATE_I, "vs")
+        for q in range(STEPS_PER_LOAD // STEPS_PER_BANK):
+            turn_x(0, q)
+            copy_x(0, q)
+        transpose_whh(GATE_G, "vs")
+        quantise_x(0)
+        make_const(GATE_I)
+        start_group(0)
+        multiply(0, GATE_I)
+        transpose_whh(GATE_F, "ss")
+        add_const(0, GATE_I)
+        make_const(GATE_G)
+        multiply(0, GATE_G)
+        activate(0, GATE_I)
+        add_const(0, GATE_G)
+        activate(0, GATE_G)
+        make_const(GATE_F)
+        mul_i_g(0)
+        multiply(0, GATE_F)
+        add_const(0, GATE_F)
+        transpose_whh(GATE_O, "ss")
+        fix_in_psum()
+        activate(0, GATE_F)
+        make_const(GATE_O)
+        mul_f_c0(0, nc.gpsimd)
+        multiply(0, GATE_O)
+        add_const(0, GATE_O)
+        activate(0, GATE_O)
+        turn_x(1, 0)
+        copy_x(1, 0)
+        mul_f_c0(0, nc.vector)
+
+        for n in range(1, GROUPS + 2):
+            here, before = n < GROUPS, n <= GROUPS
+            load, q = divmod(n + 2, 2)
+            if here:
+                start_group(n)
+                multiply(n, GATE_I)
+                add_const(n, GATE_I)
+                multiply(n, GATE_G)
+                activate(n, GATE_I)
+                add_const(n, GATE_G)
+                activate(n, GATE_G)
+                mul_i_g(n)
+                multiply(n, GATE_F)
+                add_const(n, GATE_F)
+                if load < LOADS:
+                    turn_x(load, q)
+                multiply(n, GATE_O)
             if n >= 2:
                 store_h(n - 2)
-            if 1 <= n <= GROUPS:
-                tanh_c = work.tile(group_shape, F32, name="tanh_c")
-                o_tanh_c[n - 1] = work.tile(group_shape, F32, name="o_tanh_c")
-                for steps in pieces(n - 1):
-                    nc.scalar.activation(out=tanh_c[:, steps], in_=cell[n - 1][:, steps], func=ACT.Tanh)
-                for steps in pieces(n - 1):
-                    helper(n - 1).tensor_tensor(
-                        out=o_tanh_c[n - 1][:, steps],
-                        in0=gates[n - 1][:, GATE_O, steps],
-                        in1=tanh_c[:, steps],
-                        op=ALU.mult,
-                    )
-            if n < GROUPS:
-                project(n, GATE_O)
-                if n % GROUPS_PER_LOAD == 1 and next_load < LOADS:
-                    quantise_x(next_load)
-            if n == 0:
-                fix_in_psum()
-            if n < GROUPS:
-                f_c0 = work.tile(group_shape, F32, name="f_c0")
-                nc.vector.tensor_tensor(out=f_c0[:], in0=gates[n][:, GATE_F], in1=c0_bc, op=ALU.mult)
-                cell[n] = work.tile(group_shape, F32, name="cell")
-                for steps in pieces(n):
-                    helper(n).tensor_tensor(out=cell[n][:, steps], in0=f_c0[:, steps], in1=i_g[:, steps], op=ALU.add)
-                if n == GROUPS - 1:
-                    nc.scalar.dma_start(out=out_state[1], in_=cell[n][:, STEPS_PER_GROUP - 1, :])
-            if n % GROUPS_PER_LOAD == 0 and next_load < LOADS:
-                regroup_x(next_load)
+            if before:
+                tanh_c[n - 1] = work.tile(group_shape, F32, name="tanh_c")
+                sum_cell(n - 1, 0)
+            if here:
+                if load < LOADS:
+                    copy_x(load, q)
+                activate(n, GATE_F)
+            if before:
+                sum_cell(n - 1, 1)
+                tanh_cell(n - 1, 0)
+            if here:
+                mul_f_c0(n, nc.gpsimd)
+                add_const(n, GATE_O)
+                if load < LOADS and q == 1:
+                    quantise_x(load)
+            if before:
+                tanh_cell(n - 1, 1)
+            if here:
+                activate(n, GATE_O)
+            if before:
+                mul_o(n - 1)
+            if here:
+                mul_f_c0(n, nc.vector)

@@ -21,16 +21,13 @@ GATES = 4
 GATE_I, GATE_F, GATE_G, GATE_O = 0, 1, 2, 3
 WORDS = K // 2
 STEPS_PER_LOAD = 4
-STEPS_PER_BANK = 2
-STEPS_PER_GROUP = 2
-GROUPS = STEPS // STEPS_PER_GROUP
+PAIR = 2
+GROUPS = STEPS // PAIR
 LOADS = STEPS // STEPS_PER_LOAD
-GROUPS_PER_LOAD = STEPS_PER_LOAD // STEPS_PER_GROUP
-GATE_ORDER = (GATE_I, GATE_G, GATE_F, GATE_O)
-BLOCKS_ON_VECTOR = 2
-GROUPS_WITHOUT_HELPER = 1
 BLOCKS = H // P
-BLOCKS_PER_BANK = 2
+WIDE = PAIR * H
+G_BLOCKS = 2
+G_COLS = G_BLOCKS * PAIR * P
 WARM_UP = 6
 
 FLOPS = 2 * STEPS * P * K * GATES * H + 2 * P * H * GATES * H
@@ -46,7 +43,7 @@ def tile_lstmlayer_kernel(
         stage = ctx.enter_context(tc.tile_pool(name="stage", bufs=2))
         work = ctx.enter_context(tc.tile_pool(name="work", bufs=2))
         fixed_psum = ctx.enter_context(tc.psum_pool(name="fixed_psum", bufs=1))
-        psum = ctx.enter_context(tc.psum_pool(name="psum", bufs=4))
+        psum = ctx.enter_context(tc.psum_pool(name="psum", bufs=5))
         cell_psum = ctx.enter_context(tc.psum_pool(name="cell_psum", bufs=2))
 
         ident_f32 = keep.tile([P, P], F32)
@@ -60,8 +57,10 @@ def tile_lstmlayer_kernel(
         nc.vector.memset(warm[:], 0.0)
         nc.scalar.activation(out=warm[:], in_=warm[:], func=ACT.Sigmoid)
 
-        bias_rows = keep.tile([P, GATES * H], BF16)
-        nc.vector.memset(bias_rows[:].bitcast(I32), 0)
+        bias_blocks = keep.tile([P, P], BF16)
+        nc.vector.memset(bias_blocks[:].bitcast(I32), 0)
+        bias_rows_o = keep.tile([P, H], BF16)
+        nc.vector.memset(bias_rows_o[:].bitcast(I32), 0)
         w_scale_plane = keep.tile([P, GATES * H], U8, align_bytes=64)
         nc.vector.memset(w_scale_plane[:].bitcast(I32), 0)
 
@@ -73,6 +72,7 @@ def tile_lstmlayer_kernel(
         x_scales = keep.tile([P, STEPS, P], U8, align_bytes=64)
         x_loads = []
         grouped_tiles = {}
+        x_t = {}
 
         def load_x(c):
             x_sb = keep.tile([P, STEPS_PER_LOAD, K], BF16, name="x_sb%d" % c)
@@ -82,25 +82,20 @@ def tile_lstmlayer_kernel(
             )
             x_loads.append(x_sb)
 
-        x_t = {}
-
         def turn_x(c, q):
             x_words = x_loads[c][:].rearrange("b s k -> b (s k)").bitcast(F32)
-            x_t_ps = psum.tile([P, STEPS_PER_BANK, 2, P], F32, tag="bank", name="x_t_ps")
-            for s in range(STEPS_PER_BANK):
-                first = WORDS * (STEPS_PER_BANK * q + s)
+            x_t_ps = psum.tile([P, PAIR, 2, P], F32, tag="bank", name="x_t_ps")
+            for s in range(PAIR):
+                first = WORDS * (PAIR * q + s)
                 for u in range(2):
                     nc.tensor.transpose(x_t_ps[:, s, u, :], x_words[:, first + u : first + WORDS : 2], ident_f32[:])
             x_t[c, q] = x_t_ps
 
         def copy_x(c, q):
-            if q == 0:
+            if c not in grouped_tiles:
                 grouped_tiles[c] = stage.tile([P, STEPS_PER_LOAD * P * 4], BF16, align_bytes=64, name="grouped")
             grouped_words = grouped_tiles[c][:].bitcast(F32).rearrange("p (s b u) -> p s b u", s=STEPS_PER_LOAD, u=2)
-            nc.scalar.copy(
-                out=grouped_words[:, STEPS_PER_BANK * q : STEPS_PER_BANK * (q + 1)],
-                in_=x_t[c, q][:].rearrange("p s u b -> p s b u"),
-            )
+            nc.scalar.copy(out=grouped_words[:, PAIR * q : PAIR * (q + 1)], in_=x_t[c, q][:].rearrange("p s u b -> p s b u"))
 
         def quantise_x(c):
             steps = slice(STEPS_PER_LOAD * c, STEPS_PER_LOAD * (c + 1))
@@ -111,7 +106,7 @@ def tile_lstmlayer_kernel(
             )
 
         const_o = keep.tile([P, H], F32)
-        const_t = keep.tile([P, GATES, BLOCKS, P], F32)
+        const_t = keep.tile([P, 3, BLOCKS, P], F32)
         w_words = keep.tile([P, 2 * GATES * H], U8, align_bytes=64)
         c0_sb = keep.tile([P, H], BF16)
         noise_sb = keep.tile([P, H], BF16)
@@ -125,38 +120,52 @@ def tile_lstmlayer_kernel(
             )
 
         nc.sync.dma_start(out=h0_sb[:], in_=h0)
-        load_whh(GATE_ORDER[0])
+        load_whh(GATE_I)
         load_x(0)
-        load_whh(GATE_ORDER[1])
+        load_whh(GATE_G)
+        nc.sync.dma_start(out=bias_blocks[0:16, :], in_=b_ih.rearrange("(r j) -> r j", j=P))
+        nc.sync.dma_start(out=bias_blocks[16:32, :], in_=b_hh.rearrange("(r j) -> r j", j=P))
         nc.sync.dma_start(out=w_words[:].bitcast(I32), in_=w_ih_words[0].bitcast(I32))
-        nc.sync.dma_start(out=bias_rows[0:1, :], in_=b_ih.rearrange("(o n) -> o n", o=1))
-        nc.sync.dma_start(out=bias_rows[1:2, :], in_=b_hh.rearrange("(o n) -> o n", o=1))
         for quad in range(4):
             nc.sync.dma_start(
                 out=w_scale_plane[32 * quad : 32 * quad + 4, :].bitcast(I32),
                 in_=w_ih_scales[0, 4 * quad : 4 * quad + 4, :].bitcast(I32),
             )
-        for j in GATE_ORDER[2:]:
-            load_whh(j)
+        load_whh(GATE_F)
         nc.sync.dma_start(out=c0_sb[:], in_=c0)
+        load_whh(GATE_O)
+        nc.sync.dma_start(out=bias_rows_o[0:1, :], in_=b_ih[3 * H : 4 * H].rearrange("(o n) -> o n", o=1))
+        nc.sync.dma_start(out=bias_rows_o[1:2, :], in_=b_hh[3 * H : 4 * H].rearrange("(o n) -> o n", o=1))
         nc.sync.dma_start(out=noise_sb[:], in_=noise)
         for c in range(1, LOADS):
             load_x(c)
 
-        h0_t_ps = psum.tile([P, 2, P], F32, tag="bank")
-        for half in range(2):
-            nc.tensor.transpose(
-                h0_t_ps[:, half, :], h0_sb[:].bitcast(F32)[:, P * half : P * (half + 1)], ident_f32[:]
-            )
-        h0_t = keep.tile([P, 2, P], F32)
-        nc.vector.tensor_copy(out=h0_t[:], in_=h0_t_ps[:])
         h0_rows = keep.tile([P, 2, 2, P], BF16)
-        nc.vector.tensor_copy(
-            out=h0_rows[:], in_=h0_t[:].bitcast(BF16).rearrange("w half (b e) -> w half e b", e=2)
-        )
         whh_t = keep.tile([P, 2, GATES * H], F32)
+        bias_t = keep.tile([P, GATES * BLOCKS], F32)
 
-        def transpose_whh(j, engines):
+        def turn_h0():
+            h0_t_ps = cell_psum.tile([P, 2, P], F32, tag="cell", name="h0_t_ps")
+            for half in range(2):
+                nc.tensor.transpose(
+                    h0_t_ps[:, half, :], h0_sb[:].bitcast(F32)[:, P * half : P * (half + 1)], ident_f32[:]
+                )
+            h0_t = keep.tile([P, 2, P], F32)
+            nc.vector.tensor_copy(out=h0_t[:], in_=h0_t_ps[:])
+            nc.vector.tensor_copy(
+                out=h0_rows[:], in_=h0_t[:].bitcast(BF16).rearrange("w half (b e) -> w half e b", e=2)
+            )
+
+        def turn_bias():
+            bias_ps = psum.tile([P, H], F32, tag="bank", name="bias_ps")
+            cols = GATES * BLOCKS
+            for k in range(2):
+                nc.tensor.matmul(
+                    out=bias_ps[:, 0:cols], lhsT=bias_blocks[:], rhs=ident_bf16[:, cols * k : cols * (k + 1)], start=(k == 0), stop=(k == 1)
+                )
+            nc.vector.tensor_copy(out=bias_t[:], in_=bias_ps[:, 0:cols])
+
+        def turn_whh(j, engines):
             for half in range(2):
                 whh_t_ps = cell_psum.tile([P, 4, P], F32, tag="cell", name="whh_t_ps")
                 for a in range(4):
@@ -174,64 +183,74 @@ def tile_lstmlayer_kernel(
 
         def make_const(j):
             const_ps = psum.tile([P, H], F32, tag="bank", name="const_ps")
-            if j != GATE_O:
-                for blk in range(BLOCKS):
-                    cols = slice(H * j + P * blk, H * j + P * (blk + 1))
-                    for half in range(2):
-                        for e in range(2):
-                            nc.tensor.matmul(
-                                out=const_ps[:, P * blk : P * (blk + 1)],
-                                lhsT=whh_t[:, half, cols].bitcast(BF16).rearrange("w (n e) -> w n e", e=2)[:, :, e],
-                                rhs=h0_rows[:, half, e, :],
-                                start=(half == 0 and e == 0),
-                                stop=False,
-                            )
-                    nc.tensor.matmul(
-                        out=const_ps[:, P * blk : P * (blk + 1)], lhsT=bias_rows[:, cols], rhs=ones[:], start=False, stop=True
-                    )
-                nc.vector.tensor_copy(out=const_t[:, j].rearrange("p k b -> p (k b)"), in_=const_ps[:])
+            if j == GATE_O:
+                for half in range(2):
+                    for e in range(2):
+                        nc.tensor.matmul(
+                            out=const_ps[:],
+                            lhsT=h0_rows[:, half, e, :],
+                            rhs=whh_t[:, half, H * j : H * (j + 1)].bitcast(BF16).rearrange("w (n e) -> w n e", e=2)[:, :, e],
+                            start=(half == 0 and e == 0),
+                            stop=False,
+                        )
+                nc.tensor.matmul(out=const_ps[:], lhsT=ones[:], rhs=bias_rows_o[:], start=False, stop=True)
+                nc.vector.tensor_copy(out=const_o[:], in_=const_ps[:])
                 return
-            for half in range(2):
-                for e in range(2):
-                    nc.tensor.matmul(
-                        out=const_ps[:],
-                        lhsT=h0_rows[:, half, e, :],
-                        rhs=whh_t[:, half, H * j : H * (j + 1)]
-                        .bitcast(BF16)
-                        .rearrange("w (n e) -> w n e", e=2)[:, :, e],
-                        start=(half == 0 and e == 0),
-                        stop=False,
-                    )
-            nc.tensor.matmul(
-                out=const_ps[:], lhsT=ones[:], rhs=bias_rows[:, H * j : H * (j + 1)], start=False, stop=True
-            )
-            nc.vector.tensor_copy(out=const_o[:], in_=const_ps[:])
+            for blk in range(BLOCKS):
+                cols = slice(H * j + P * blk, H * j + P * (blk + 1))
+                for half in range(2):
+                    for e in range(2):
+                        nc.tensor.matmul(
+                            out=const_ps[:, P * blk : P * (blk + 1)],
+                            lhsT=whh_t[:, half, cols].bitcast(BF16).rearrange("w (n e) -> w n e", e=2)[:, :, e],
+                            rhs=h0_rows[:, half, e, :],
+                            start=(half == 0 and e == 0),
+                            stop=(half == 1 and e == 1),
+                        )
+            for blk in range(BLOCKS):
+                place = BLOCKS * j + blk
+                nc.vector.tensor_scalar(
+                    out=const_t[:, j, blk, :],
+                    in0=const_ps[:, P * blk : P * (blk + 1)],
+                    scalar1=bias_t[:, place : place + 1],
+                    scalar2=None,
+                    op0=ALU.add,
+                )
 
-
-        c0_ps = fixed_psum.tile([P, BLOCKS, P], F32)
-        c0_t = keep.tile([P, BLOCKS - BLOCKS_ON_VECTOR, P], F32)
-        noise_ps = fixed_psum.tile([P, H], F32)
+        fixed_ps = fixed_psum.tile([P, 2, H], BF16)
+        c0_ps = fixed_ps[:, 0].rearrange("p (k b) -> p k b", k=BLOCKS)
+        noise_ps = fixed_ps[:, 1]
+        c0_t = keep.tile([P, G_BLOCKS, P], F32)
+        times = [keep.tile([P, WIDE + G_COLS], F32, name="times%d" % m) for m in range(2)]
 
         def fix_in_psum():
             for blk in range(BLOCKS):
-                nc.tensor.matmul(
-                    out=c0_ps[:, blk, :], lhsT=c0_sb[:, P * blk : P * (blk + 1)], rhs=ident_bf16[:], start=True, stop=True
+                nc.tensor.transpose(c0_ps[:, blk, :], c0_sb[:, P * blk : P * (blk + 1)], ident_bf16[:])
+            nc.tensor.matmul(out=noise_ps, lhsT=ident_bf16[:], rhs=noise_sb[:], start=True, stop=True)
+            nc.scalar.copy(out=c0_t[:], in_=c0_ps[:, 0:G_BLOCKS, :])
+            for m in range(2):
+                nc.gpsimd.tensor_scalar(
+                    out=times[m][:, WIDE:].rearrange("p (k s b) -> p k s b", k=G_BLOCKS, s=PAIR),
+                    in0=c0_t[:].unsqueeze(2).to_broadcast([P, G_BLOCKS, PAIR, P]),
+                    scalar1=1.0,
+                    scalar2=0.0,
+                    op0=ALU.mult,
+                    op1=ALU.add,
                 )
-            nc.scalar.copy(out=c0_t[:], in_=c0_ps[:, BLOCKS_ON_VECTOR:BLOCKS, :])
-            nc.tensor.matmul(out=noise_ps[:], lhsT=ident_bf16[:], rhs=noise_sb[:], start=True, stop=True)
 
-        group_shape = [P, STEPS_PER_GROUP, H]
-        turned = "p (k s b) -> p k s b"
-        noise_bc = noise_ps[:].unsqueeze(1).to_broadcast(group_shape)
-        gates, i_gs, f_c0s, cell, o_tanh_c = {}, {}, {}, {}, {}
+        group_shape = [P, PAIR, H]
+        noise_bc = noise_ps.unsqueeze(1).to_broadcast(group_shape)
+        i_f, o_gate, products, cell, tanh_c, o_tanh_c, banks = {}, {}, {}, {}, {}, {}, {}
 
-        def turned_view(tile_2d):
-            return tile_2d.rearrange(turned, k=BLOCKS, s=STEPS_PER_GROUP)
-
-        banks = {}
+        def gate_columns(n, gate):
+            if gate == GATE_O:
+                return o_gate[n][:]
+            if gate == GATE_G:
+                return times[n % 2][:, 0:WIDE]
+            return i_f[n][:, WIDE * gate : WIDE * (gate + 1)]
 
         def multiply(n, gate):
-            first = STEPS_PER_GROUP * n
+            first = PAIR * n
             for bank in range(2):
                 if gate == GATE_O:
                     gate_ps = psum.tile([P, H], F32, tag="bank", name="gate_ps")
@@ -245,15 +264,15 @@ def tile_lstmlayer_kernel(
                         stop=True,
                     )
                 else:
-                    gate_ps = psum.tile([P, BLOCKS_PER_BANK, STEPS_PER_GROUP, P], F32, tag="bank", name="gate_ps")
-                    for k in range(BLOCKS_PER_BANK):
-                        col = H * gate + P * (BLOCKS_PER_BANK * bank + k)
+                    gate_ps = psum.tile([P, 2, PAIR, P], F32, tag="bank", name="gate_ps")
+                    for k in range(2):
+                        col = H * gate + P * (2 * bank + k)
                         nc.tensor.matmul_mx(
                             out=gate_ps[:, k].rearrange("p s b -> p (s b)"),
                             lhsT=w_words[:, 2 * col : 2 * (col + P)].bitcast(FP4X4),
                             lhsT_scale=w_scale_plane[:, col : col + P],
-                            rhs=x_codes[:, first : first + STEPS_PER_GROUP, :].rearrange("p s b -> p (s b)").bitcast(FP8X4),
-                            rhs_scale=x_scales[:, first : first + STEPS_PER_GROUP, :].rearrange("p s b -> p (s b)"),
+                            rhs=x_codes[:, first : first + PAIR, :].rearrange("p s b -> p (s b)").bitcast(FP8X4),
+                            rhs_scale=x_scales[:, first : first + PAIR, :].rearrange("p s b -> p (s b)"),
                             start=True,
                             stop=True,
                         )
@@ -261,56 +280,59 @@ def tile_lstmlayer_kernel(
 
         def add_const(n, gate):
             for bank in range(2):
-                gate_ps = banks[n, gate, bank]
+                half = gate_columns(n, gate)[:, H * bank : H * (bank + 1)]
                 if gate == GATE_O:
-                    nc.vector.tensor_tensor(
-                        out=gates[n][:, gate, H * bank : H * (bank + 1)], in0=gate_ps[:], in1=const_o[:], op=ALU.add
-                    )
+                    nc.vector.tensor_tensor(out=half, in0=banks[n, gate, bank][:], in1=const_o[:], op=ALU.add)
                 else:
-                    blocks = slice(BLOCKS_PER_BANK * bank, BLOCKS_PER_BANK * (bank + 1))
                     nc.vector.tensor_tensor(
-                        out=turned_view(gates[n][:, gate])[:, blocks],
-                        in0=gate_ps[:],
-                        in1=const_t[:, gate, blocks, :].unsqueeze(2).to_broadcast([P, BLOCKS_PER_BANK, STEPS_PER_GROUP, P]),
+                        out=half.rearrange("p (k s b) -> p k s b", k=2, s=PAIR),
+                        in0=banks[n, gate, bank][:],
+                        in1=const_t[:, gate, 2 * bank : 2 * bank + 2, :].unsqueeze(2).to_broadcast([P, 2, PAIR, P]),
                         op=ALU.add,
                     )
 
         def activate(n, gate):
-            nc.scalar.activation(
-                out=gates[n][:, gate],
-                in_=gates[n][:, gate],
-                func=(ACT.Tanh if gate == GATE_G else ACT.Sigmoid),
+            columns = gate_columns(n, gate)
+            nc.scalar.activation(out=columns, in_=columns, func=(ACT.Tanh if gate == GATE_G else ACT.Sigmoid))
+
+        def start_group(n):
+            i_f[n] = work.tile([P, 2 * WIDE], F32, bufs=3, name="i_f")
+            o_gate[n] = work.tile([P, WIDE], F32, bufs=3, name="o_gate")
+            products[n] = work.tile([P, 2, BLOCKS, PAIR, P], F32, bufs=2, name="products")
+
+        def multiply_i_g_and_f_c0(n):
+            if n == GROUPS - 1:
+                nc.gpsimd.tensor_tensor(
+                    out=products[n][:, 0].rearrange("p k s b -> p (k s b)"),
+                    in0=i_f[n][:, 0:WIDE],
+                    in1=times[n % 2][:, 0:WIDE],
+                    op=ALU.mult,
+                )
+                return
+            nc.gpsimd.tensor_tensor(
+                out=products[n][:].rearrange("p h k s b -> p (h k s b)")[:, 0 : WIDE + G_COLS],
+                in0=i_f[n][:, 0 : WIDE + G_COLS],
+                in1=times[n % 2][:],
+                op=ALU.mult,
             )
 
-        def helper(n):
-            return nc.vector if n >= GROUPS - GROUPS_WITHOUT_HELPER else nc.gpsimd
-
-        def pieces(n):
-            if n < GROUPS - 1:
-                return [slice(0, STEPS_PER_GROUP)]
-            return [slice(s, s + 1) for s in range(STEPS_PER_GROUP)]
-
-        def store_h(n):
-            h = work.tile(group_shape, F32, name="h")
-            for steps in pieces(n):
-                nc.vector.tensor_tensor(
-                    out=h[:, steps], in0=o_tanh_c[n][:, steps], in1=noise_bc[:, steps], op=ALU.add
-                )
-                first = STEPS_PER_GROUP * n
-                nc.sync.dma_start(
-                    out=out_h[first + steps.start : first + steps.stop].rearrange("t b m -> b t m"),
-                    in_=h[:, steps],
-                )
-            if n == GROUPS - 1:
-                nc.scalar.dma_start(out=out_state[0], in_=h[:, STEPS_PER_GROUP - 1, :])
+        def multiply_f_c0(n):
+            skip = G_BLOCKS if n < GROUPS - 1 else 0
+            count = BLOCKS - skip
+            nc.vector.tensor_tensor(
+                out=products[n][:, 1, skip:],
+                in0=i_f[n][:, WIDE + skip * PAIR * P :].rearrange("p (k s b) -> p k s b", k=count, s=PAIR),
+                in1=c0_ps[:, skip:, :].unsqueeze(2).to_broadcast([P, count, PAIR, P]),
+                op=ALU.mult,
+            )
 
         def sum_cell(n, s):
             c_ps = cell_psum.tile([P, BLOCKS, P], F32, tag="cell", name="c_ps")
-            for k, product in enumerate((i_gs[n], f_c0s[n])):
+            for k in range(2):
                 for blk in range(BLOCKS):
                     nc.tensor.matmul(
                         out=c_ps[:, blk, :],
-                        lhsT=product[:, blk, s, :],
+                        lhsT=products[n][:, k, blk, s, :],
                         rhs=ident_f32[:],
                         is_transpose=True,
                         start=(k == 0 and blk == 0),
@@ -319,123 +341,112 @@ def tile_lstmlayer_kernel(
             cell[n, s] = c_ps
 
         def tanh_cell(n, s):
-            nc.scalar.activation(
-                out=tanh_c[n][:, s], in_=cell[n, s][:].rearrange("p k b -> p (k b)"), func=ACT.Tanh
-            )
-            if n == GROUPS - 1 and s == STEPS_PER_GROUP - 1:
+            if s == 0:
+                tanh_c[n] = work.tile(group_shape, F32, name="tanh_c")
+            c_row = cell[n, s][:].rearrange("p k b -> p (k b)")
+            nc.scalar.activation(out=tanh_c[n][:, s], in_=c_row, func=ACT.Tanh)
+            if n == GROUPS - 1 and s == PAIR - 1:
                 c_last = keep.tile([P, H], F32)
-                nc.scalar.copy(out=c_last[:], in_=cell[n, s][:].rearrange("p k b -> p (k b)"))
+                nc.scalar.copy(out=c_last[:], in_=c_row)
                 nc.scalar.dma_start(out=out_state[1], in_=c_last[:])
 
-        turned_shape = [P, BLOCKS, STEPS_PER_GROUP, P]
-        tanh_c = {}
+        def pieces(n):
+            if n < GROUPS - 1:
+                return [slice(0, PAIR)]
+            return [slice(s, s + 1) for s in range(PAIR)]
 
-        def mul_i_g(n):
-            i_gs[n] = work.tile(turned_shape, F32, name="i_g")
-            nc.gpsimd.tensor_tensor(
-                out=i_gs[n][:],
-                in0=turned_view(gates[n][:, GATE_I]),
-                in1=turned_view(gates[n][:, GATE_G]),
-                op=ALU.mult,
-            )
-
-        def mul_f_c0(n, engine):
-            if n not in f_c0s:
-                f_c0s[n] = work.tile(turned_shape, F32, name="f_c0")
-            mine = slice(0, BLOCKS_ON_VECTOR) if engine == nc.vector else slice(BLOCKS_ON_VECTOR, BLOCKS)
-            count = mine.stop - mine.start
-            source = c0_ps[:, mine, :] if engine == nc.vector else c0_t[:]
-            engine.tensor_tensor(
-                out=f_c0s[n][:, mine],
-                in0=turned_view(gates[n][:, GATE_F])[:, mine],
-                in1=source.unsqueeze(2).to_broadcast([P, count, STEPS_PER_GROUP, P]),
-                op=ALU.mult,
-            )
-
-        def mul_o(n):
+        def multiply_o(n):
             o_tanh_c[n] = work.tile(group_shape, F32, name="o_tanh_c")
+            engine = nc.vector if n == GROUPS - 1 else nc.gpsimd
             for steps in pieces(n):
-                helper(n).tensor_tensor(
+                engine.tensor_tensor(
                     out=o_tanh_c[n][:, steps],
-                    in0=gates[n][:, GATE_O].rearrange("p (s m) -> p s m", s=STEPS_PER_GROUP)[:, steps],
+                    in0=o_gate[n][:].rearrange("p (s m) -> p s m", s=PAIR)[:, steps],
                     in1=tanh_c[n][:, steps],
                     op=ALU.mult,
                 )
 
-        def start_group(n):
-            gates[n] = work.tile([P, GATES, STEPS_PER_GROUP * H], F32, bufs=4, name="gates")
+        def store_h(n):
+            h = work.tile(group_shape, F32, name="h")
+            for steps in pieces(n):
+                nc.vector.tensor_tensor(out=h[:, steps], in0=o_tanh_c[n][:, steps], in1=noise_bc[:, steps], op=ALU.add)
+                first = PAIR * n
+                nc.sync.dma_start(
+                    out=out_h[first + steps.start : first + steps.stop].rearrange("t b m -> b t m"),
+                    in_=h[:, steps],
+                )
+            if n == GROUPS - 1:
+                nc.scalar.dma_start(out=out_state[0], in_=h[:, PAIR - 1, :])
 
-        transpose_whh(GATE_I, "vs")
-        for q in range(STEPS_PER_LOAD // STEPS_PER_BANK):
-            turn_x(0, q)
-            copy_x(0, q)
-        transpose_whh(GATE_G, "vs")
+        turn_h0()
+        turn_whh(GATE_I, "vs")
+        turn_x(0, 0)
+        copy_x(0, 0)
+        turn_x(0, 1)
+        copy_x(0, 1)
+        turn_bias()
         quantise_x(0)
         make_const(GATE_I)
+        turn_whh(GATE_G, "vs")
         start_group(0)
         multiply(0, GATE_I)
-        transpose_whh(GATE_F, "ss")
-        add_const(0, GATE_I)
         make_const(GATE_G)
+        turn_whh(GATE_F, "ss")
+        add_const(0, GATE_I)
         multiply(0, GATE_G)
         activate(0, GATE_I)
         add_const(0, GATE_G)
         activate(0, GATE_G)
         make_const(GATE_F)
-        mul_i_g(0)
+        turn_whh(GATE_O, "ss")
+        fix_in_psum()
         multiply(0, GATE_F)
         add_const(0, GATE_F)
-        transpose_whh(GATE_O, "ss")
-        fix_in_psum()
         activate(0, GATE_F)
+        multiply_i_g_and_f_c0(0)
         make_const(GATE_O)
-        mul_f_c0(0, nc.gpsimd)
         multiply(0, GATE_O)
         add_const(0, GATE_O)
         activate(0, GATE_O)
         turn_x(1, 0)
         copy_x(1, 0)
-        mul_f_c0(0, nc.vector)
+        multiply_f_c0(0)
 
         for n in range(1, GROUPS + 2):
             here, before = n < GROUPS, n <= GROUPS
             load, q = divmod(n + 2, 2)
+            if load < LOADS:
+                turn_x(load, q)
             if here:
                 start_group(n)
                 multiply(n, GATE_I)
                 add_const(n, GATE_I)
-                multiply(n, GATE_G)
+            if load < LOADS:
+                copy_x(load, q)
+            if here:
                 activate(n, GATE_I)
+                multiply(n, GATE_G)
                 add_const(n, GATE_G)
                 activate(n, GATE_G)
-                mul_i_g(n)
                 multiply(n, GATE_F)
                 add_const(n, GATE_F)
-                if load < LOADS:
-                    turn_x(load, q)
                 multiply(n, GATE_O)
-            if n >= 2:
-                store_h(n - 2)
-            if before:
-                tanh_c[n - 1] = work.tile(group_shape, F32, name="tanh_c")
-                sum_cell(n - 1, 0)
-            if here:
-                if load < LOADS:
-                    copy_x(load, q)
                 activate(n, GATE_F)
             if before:
+                sum_cell(n - 1, 0)
                 sum_cell(n - 1, 1)
                 tanh_cell(n - 1, 0)
             if here:
-                mul_f_c0(n, nc.gpsimd)
+                multiply_i_g_and_f_c0(n)
                 add_const(n, GATE_O)
-                if load < LOADS and q == 1:
-                    quantise_x(load)
             if before:
                 tanh_cell(n - 1, 1)
+            if load < LOADS and q == 1:
+                quantise_x(load)
+            if n >= 2:
+                store_h(n - 2)
             if here:
+                multiply_f_c0(n)
                 activate(n, GATE_O)
             if before:
-                mul_o(n - 1)
-            if here:
-                mul_f_c0(n, nc.vector)
+                multiply_o(n - 1)

@@ -28,6 +28,9 @@ BLOCKS = H // P
 WIDE = PAIR * H
 G_BLOCKS = 2
 G_COLS = G_BLOCKS * PAIR * P
+ALONE = (15,)
+MO_V = 14
+LOAD_ORDER = (0, 1, 2, 3, 4, 5, 7, 6)
 WARM_UP = 6
 
 FLOPS = 2 * STEPS * P * K * GATES * H + 2 * P * H * GATES * H
@@ -64,9 +67,12 @@ def tile_lstmlayer_kernel(
         w_scale_plane = keep.tile([P, GATES * H], U8, align_bytes=64)
         nc.vector.memset(w_scale_plane[:].bitcast(I32), 0)
 
-        warm_ps = psum.tile([P, H], F32, tag="bank", name="warm_ps")
-        for k in range(WARM_UP):
-            nc.tensor.matmul(out=warm_ps[:, 0:P], lhsT=ident_f32[:], rhs=ident_f32[:], start=True, stop=True)
+        def warm_tensor(count):
+            warm_ps = psum.tile([P, H], F32, tag="bank", name="warm_ps")
+            for k in range(count):
+                nc.tensor.matmul(out=warm_ps[:, 0:P], lhsT=ident_f32[:], rhs=ident_f32[:], start=True, stop=True)
+
+        warm_tensor(WARM_UP)
 
         x_codes = keep.tile([P, STEPS, P], U32, align_bytes=64)
         x_scales = keep.tile([P, STEPS, P], U8, align_bytes=64)
@@ -74,12 +80,14 @@ def tile_lstmlayer_kernel(
         grouped_tiles = {}
         x_t = {}
 
+        def first_step(n):
+            load, q = divmod(PAIR * n, STEPS_PER_LOAD)
+            return STEPS_PER_LOAD * LOAD_ORDER[load] + q
+
         def load_x(c):
             x_sb = keep.tile([P, STEPS_PER_LOAD, K], BF16, name="x_sb%d" % c)
-            nc.sync.dma_start(
-                out=x_sb[:],
-                in_=x[STEPS_PER_LOAD * c : STEPS_PER_LOAD * (c + 1)].rearrange("t b k -> b t k"),
-            )
+            first = first_step(c * STEPS_PER_LOAD // PAIR)
+            nc.sync.dma_start(out=x_sb[:], in_=x[first : first + STEPS_PER_LOAD].rearrange("t b k -> b t k"))
             x_loads.append(x_sb)
 
         def turn_x(c, q):
@@ -119,12 +127,19 @@ def tile_lstmlayer_kernel(
                 in_=w_hh[H * j : H * (j + 1), :].rearrange("(p a) k -> p a k", a=4),
             )
 
+        def load_whh_half(j, pair):
+            rows = slice(H * j + 2 * P * pair, H * j + 2 * P * (pair + 1))
+            nc.sync.dma_start(
+                out=whh_sb[:, j, 2 * pair : 2 * pair + 2], in_=w_hh[rows, :].rearrange("(a p) k -> p a k", p=P)
+            )
+
+        load_whh_half(GATE_I, 0)
         nc.sync.dma_start(out=h0_sb[:], in_=h0)
-        load_whh(GATE_I)
+        load_whh_half(GATE_I, 1)
         load_x(0)
-        load_whh(GATE_G)
         nc.sync.dma_start(out=bias_blocks[0:16, :], in_=b_ih.rearrange("(r j) -> r j", j=P))
         nc.sync.dma_start(out=bias_blocks[16:32, :], in_=b_hh.rearrange("(r j) -> r j", j=P))
+        load_whh(GATE_G)
         nc.sync.dma_start(out=w_words[:].bitcast(I32), in_=w_ih_words[0].bitcast(I32))
         for quad in range(4):
             nc.sync.dma_start(
@@ -165,7 +180,27 @@ def tile_lstmlayer_kernel(
                 )
             nc.vector.tensor_copy(out=bias_t[:], in_=bias_ps[:, 0:cols])
 
+        def turn_whh_pairs(j, engines):
+            for pair in range(2):
+                whh_t_ps = cell_psum.tile([P, 2, 2, P], F32, tag="cell", name="whh_t_ps")
+                for a in range(2):
+                    for half in range(2):
+                        nc.tensor.transpose(
+                            whh_t_ps[:, half, a, :],
+                            whh_sb[:, j, 2 * pair + a, :].bitcast(F32)[:, P * half : P * (half + 1)],
+                            ident_f32[:],
+                        )
+                first = H * j + 2 * P * pair
+                dst = whh_t[:, :, first : first + 2 * P]
+                src = whh_t_ps[:].rearrange("w h a p -> w h (a p)")
+                if engines[pair] == "v":
+                    nc.vector.tensor_copy(out=dst, in_=src)
+                else:
+                    nc.scalar.copy(out=dst, in_=src)
+
         def turn_whh(j, engines):
+            if j == GATE_I:
+                return turn_whh_pairs(j, engines)
             for half in range(2):
                 whh_t_ps = cell_psum.tile([P, 4, P], F32, tag="cell", name="whh_t_ps")
                 for a in range(4):
@@ -181,8 +216,15 @@ def tile_lstmlayer_kernel(
                 else:
                     nc.scalar.copy(out=dst, in_=src)
 
+        const_banks = {}
+
         def make_const(j):
+            multiply_h0(j)
+            copy_const(j)
+
+        def multiply_h0(j):
             const_ps = psum.tile([P, H], F32, tag="bank", name="const_ps")
+            const_banks[j] = const_ps
             if j == GATE_O:
                 for half in range(2):
                     for e in range(2):
@@ -194,7 +236,6 @@ def tile_lstmlayer_kernel(
                             stop=False,
                         )
                 nc.tensor.matmul(out=const_ps[:], lhsT=ones[:], rhs=bias_rows_o[:], start=False, stop=True)
-                nc.vector.tensor_copy(out=const_o[:], in_=const_ps[:])
                 return
             for blk in range(BLOCKS):
                 cols = slice(H * j + P * blk, H * j + P * (blk + 1))
@@ -207,6 +248,12 @@ def tile_lstmlayer_kernel(
                             start=(half == 0 and e == 0),
                             stop=(half == 1 and e == 1),
                         )
+
+        def copy_const(j):
+            const_ps = const_banks[j]
+            if j == GATE_O:
+                nc.vector.tensor_copy(out=const_o[:], in_=const_ps[:])
+                return
             for blk in range(BLOCKS):
                 place = BLOCKS * j + blk
                 nc.vector.tensor_scalar(
@@ -301,7 +348,7 @@ def tile_lstmlayer_kernel(
             products[n] = work.tile([P, 2, BLOCKS, PAIR, P], F32, bufs=2, name="products")
 
         def multiply_i_g_and_f_c0(n):
-            if n == GROUPS - 1:
+            if n in ALONE:
                 nc.gpsimd.tensor_tensor(
                     out=products[n][:, 0].rearrange("p k s b -> p (k s b)"),
                     in0=i_f[n][:, 0:WIDE],
@@ -316,8 +363,16 @@ def tile_lstmlayer_kernel(
                 op=ALU.mult,
             )
 
+        def multiply_i_g_alone(n):
+            nc.gpsimd.tensor_tensor(
+                out=products[n][:, 0].rearrange("p k s b -> p (k s b)"),
+                in0=i_f[n][:, 0:WIDE],
+                in1=times[n % 2][:, 0:WIDE],
+                op=ALU.mult,
+            )
+
         def multiply_f_c0(n):
-            skip = G_BLOCKS if n < GROUPS - 1 else 0
+            skip = G_BLOCKS if n not in ALONE else 0
             count = BLOCKS - skip
             nc.vector.tensor_tensor(
                 out=products[n][:, 1, skip:],
@@ -345,7 +400,7 @@ def tile_lstmlayer_kernel(
                 tanh_c[n] = work.tile(group_shape, F32, name="tanh_c")
             c_row = cell[n, s][:].rearrange("p k b -> p (k b)")
             nc.scalar.activation(out=tanh_c[n][:, s], in_=c_row, func=ACT.Tanh)
-            if n == GROUPS - 1 and s == PAIR - 1:
+            if first_step(n) + s == STEPS - 1:
                 c_last = keep.tile([P, H], F32)
                 nc.scalar.copy(out=c_last[:], in_=c_row)
                 nc.scalar.dma_start(out=out_state[1], in_=c_last[:])
@@ -357,7 +412,7 @@ def tile_lstmlayer_kernel(
 
         def multiply_o(n):
             o_tanh_c[n] = work.tile(group_shape, F32, name="o_tanh_c")
-            engine = nc.vector if n == GROUPS - 1 else nc.gpsimd
+            engine = nc.vector if n >= MO_V else nc.gpsimd
             for steps in pieces(n):
                 engine.tensor_tensor(
                     out=o_tanh_c[n][:, steps],
@@ -370,15 +425,16 @@ def tile_lstmlayer_kernel(
             h = work.tile(group_shape, F32, name="h")
             for steps in pieces(n):
                 nc.vector.tensor_tensor(out=h[:, steps], in0=o_tanh_c[n][:, steps], in1=noise_bc[:, steps], op=ALU.add)
-                first = PAIR * n
+                first = first_step(n)
                 nc.sync.dma_start(
                     out=out_h[first + steps.start : first + steps.stop].rearrange("t b m -> b t m"),
                     in_=h[:, steps],
                 )
-            if n == GROUPS - 1:
+            if first_step(n) + PAIR == STEPS:
                 nc.scalar.dma_start(out=out_state[0], in_=h[:, PAIR - 1, :])
 
         turn_h0()
+        warm_tensor(2)
         turn_whh(GATE_I, "vs")
         turn_x(0, 0)
         copy_x(0, 0)
@@ -390,9 +446,9 @@ def tile_lstmlayer_kernel(
         turn_whh(GATE_G, "vs")
         start_group(0)
         multiply(0, GATE_I)
+        add_const(0, GATE_I)
         make_const(GATE_G)
         turn_whh(GATE_F, "ss")
-        add_const(0, GATE_I)
         multiply(0, GATE_G)
         activate(0, GATE_I)
         add_const(0, GATE_G)
@@ -413,8 +469,10 @@ def tile_lstmlayer_kernel(
         multiply_f_c0(0)
 
         for n in range(1, GROUPS + 2):
-            here, before = n < GROUPS, n <= GROUPS
+            here, before = n < GROUPS, 1 <= n <= GROUPS
             load, q = divmod(n + 2, 2)
+            if n == GROUPS:
+                warm_tensor(6)
             if load < LOADS:
                 turn_x(load, q)
             if here:

from contextlib import ExitStack

import concourse.mybir as mybir
from concourse.masks import make_identity

F32 = mybir.dt.float32
BF16 = mybir.dt.bfloat16
I32 = mybir.dt.int32
U8 = mybir.dt.uint8
U32 = mybir.dt.uint32
FP8X4 = mybir.dt.float8_e4m3fn_x4
FP4X4 = mybir.dt.float4_e2m1fn_x4
ACT = mybir.ActivationFunctionType
ALU = mybir.AluOpType

P = 128
STEPS = 32
K = 512
H = 512
GATES = 4
GATE_I, GATE_F, GATE_G, GATE_O = 0, 1, 2, 3
WORDS = K // 2
STEPS_PER_LOAD = 4
PAIR = 2
GROUPS = STEPS // PAIR
LOADS = STEPS // STEPS_PER_LOAD
BLOCKS = H // P
WIDE = PAIR * H
G_BLOCKS = 2
G_COLS = G_BLOCKS * PAIR * P
ALONE = (15,)
MO_V = 14
LOAD_ORDER = (0, 1, 2, 3, 4, 5, 7, 6)
WARM_UP = 6

FLOPS = 2 * STEPS * P * K * GATES * H + 2 * P * H * GATES * H


def tile_lstmlayer_kernel(
    tc, x, h0, c0, noise, w_ih_words, w_ih_scales, w_hh, b_ih, b_hh, out_h, out_state
):
    nc = tc.nc
    with ExitStack() as ctx:
        ctx.enter_context(tc.manual_schedule())
        keep = ctx.enter_context(tc.tile_pool(name="keep", bufs=1))
        stage = ctx.enter_context(tc.tile_pool(name="stage", bufs=2))
        work = ctx.enter_context(tc.tile_pool(name="work", bufs=2))
        fixed_psum = ctx.enter_context(tc.psum_pool(name="fixed_psum", bufs=1))
        psum = ctx.enter_context(tc.psum_pool(name="psum", bufs=5))
        cell_psum = ctx.enter_context(tc.psum_pool(name="cell_psum", bufs=2))

        ident_f32 = keep.tile([P, P], F32)
        make_identity(nc, ident_f32[:])
        ident_bf16 = keep.tile([P, P], BF16)
        make_identity(nc, ident_bf16[:])
        ones = keep.tile([P, P], BF16)
        nc.gpsimd.memset(ones[:], 1.0)

        warm = keep.tile([P, 1], F32)
        nc.vector.memset(warm[:], 0.0)
        nc.scalar.activation(out=warm[:], in_=warm[:], func=ACT.Sigmoid)

        bias_blocks = keep.tile([P, P], BF16)
        nc.vector.memset(bias_blocks[:].bitcast(I32), 0)
        bias_rows_o = keep.tile([P, H], BF16)
        nc.vector.memset(bias_rows_o[:].bitcast(I32), 0)
        w_scale_plane = keep.tile([P, GATES * H], U8, align_bytes=64)
        nc.vector.memset(w_scale_plane[:].bitcast(I32), 0)

        def warm_tensor(count):
            warm_ps = psum.tile([P, H], F32, tag="bank", name="warm_ps")
            for k in range(count):
                nc.tensor.matmul(out=warm_ps[:, 0:P], lhsT=ident_f32[:], rhs=ident_f32[:], start=True, stop=True)

        warm_tensor(WARM_UP)

        x_codes = keep.tile([P, STEPS, P], U32, align_bytes=64)
        x_scales = keep.tile([P, STEPS, P], U8, align_bytes=64)
        x_loads = []
        grouped_tiles = {}
        x_t = {}

        def first_step(n):
            load, q = divmod(PAIR * n, STEPS_PER_LOAD)
            return STEPS_PER_LOAD * LOAD_ORDER[load] + q

        def load_x(c):
            x_sb = keep.tile([P, STEPS_PER_LOAD, K], BF16, name="x_sb%d" % c)
            first = first_step(c * STEPS_PER_LOAD // PAIR)
            nc.sync.dma_start(out=x_sb[:], in_=x[first : first + STEPS_PER_LOAD].rearrange("t b k -> b t k"))
            x_loads.append(x_sb)

        def turn_x(c, q):
            x_words = x_loads[c][:].rearrange("b s k -> b (s k)").bitcast(F32)
            x_t_ps = psum.tile([P, PAIR, 2, P], F32, tag="bank", name="x_t_ps")
            for s in range(PAIR):
                first = WORDS * (PAIR * q + s)
                for u in range(2):
                    nc.tensor.transpose(x_t_ps[:, s, u, :], x_words[:, first + u : first + WORDS : 2], ident_f32[:])
            x_t[c, q] = x_t_ps

        def copy_x(c, q):
            if c not in grouped_tiles:
                grouped_tiles[c] = stage.tile([P, STEPS_PER_LOAD * P * 4], BF16, align_bytes=64, name="grouped")
            grouped_words = grouped_tiles[c][:].bitcast(F32).rearrange("p (s b u) -> p s b u", s=STEPS_PER_LOAD, u=2)
            nc.scalar.copy(out=grouped_words[:, PAIR * q : PAIR * (q + 1)], in_=x_t[c, q][:].rearrange("p s u b -> p s b u"))

        def quantise_x(c):
            steps = slice(STEPS_PER_LOAD * c, STEPS_PER_LOAD * (c + 1))
            nc.vector.quantize_mx(
                out=x_codes[:, steps, :].rearrange("p s b -> p (s b)").bitcast(FP8X4),
                scales=x_scales[:, steps, :].rearrange("p s b -> p (s b)"),
                in_=grouped_tiles[c][:],
            )

        const_o = keep.tile([P, H], F32)
        const_t = keep.tile([P, 3, BLOCKS, P], F32)
        w_words = keep.tile([P, 2 * GATES * H], U8, align_bytes=64)
        c0_sb = keep.tile([P, H], BF16)
        noise_sb = keep.tile([P, H], BF16)
        h0_sb = keep.tile([P, H], BF16)
        whh_sb = keep.tile([P, GATES, 4, H], BF16)

        def load_whh(j):
            nc.sync.dma_start(
                out=whh_sb[:, j],
                in_=w_hh[H * j : H * (j + 1), :].rearrange("(p a) k -> p a k", a=4),
            )

        def load_whh_half(j, pair):
            rows = slice(H * j + 2 * P * pair, H * j + 2 * P * (pair + 1))
            nc.sync.dma_start(
                out=whh_sb[:, j, 2 * pair : 2 * pair + 2], in_=w_hh[rows, :].rearrange("(a p) k -> p a k", p=P)
            )

        load_whh_half(GATE_I, 0)
        nc.sync.dma_start(out=h0_sb[:], in_=h0)
        load_whh_half(GATE_I, 1)
        load_x(0)
        nc.sync.dma_start(out=bias_blocks[0:16, :], in_=b_ih.rearrange("(r j) -> r j", j=P))
        nc.sync.dma_start(out=bias_blocks[16:32, :], in_=b_hh.rearrange("(r j) -> r j", j=P))
        load_whh(GATE_G)
        nc.sync.dma_start(out=w_words[:].bitcast(I32), in_=w_ih_words[0].bitcast(I32))
        for quad in range(4):
            nc.sync.dma_start(
                out=w_scale_plane[32 * quad : 32 * quad + 4, :].bitcast(I32),
                in_=w_ih_scales[0, 4 * quad : 4 * quad + 4, :].bitcast(I32),
            )
        load_whh(GATE_F)
        nc.sync.dma_start(out=c0_sb[:], in_=c0)
        load_whh(GATE_O)
        nc.sync.dma_start(out=bias_rows_o[0:1, :], in_=b_ih[3 * H : 4 * H].rearrange("(o n) -> o n", o=1))
        nc.sync.dma_start(out=bias_rows_o[1:2, :], in_=b_hh[3 * H : 4 * H].rearrange("(o n) -> o n", o=1))
        nc.sync.dma_start(out=noise_sb[:], in_=noise)
        for c in range(1, LOADS):
            load_x(c)

        h0_rows = keep.tile([P, 2, 2, P], BF16)
        whh_t = keep.tile([P, 2, GATES * H], F32)
        bias_t = keep.tile([P, GATES * BLOCKS], F32)

        def turn_h0():
            h0_t_ps = cell_psum.tile([P, 2, P], F32, tag="cell", name="h0_t_ps")
            for half in range(2):
                nc.tensor.transpose(
                    h0_t_ps[:, half, :], h0_sb[:].bitcast(F32)[:, P * half : P * (half + 1)], ident_f32[:]
                )
            h0_t = keep.tile([P, 2, P], F32)
            nc.vector.tensor_copy(out=h0_t[:], in_=h0_t_ps[:])
            nc.vector.tensor_copy(
                out=h0_rows[:], in_=h0_t[:].bitcast(BF16).rearrange("w half (b e) -> w half e b", e=2)
            )

        def turn_bias():
            bias_ps = psum.tile([P, H], F32, tag="bank", name="bias_ps")
            cols = GATES * BLOCKS
            for k in range(2):
                nc.tensor.matmul(
                    out=bias_ps[:, 0:cols], lhsT=bias_blocks[:], rhs=ident_bf16[:, cols * k : cols * (k + 1)], start=(k == 0), stop=(k == 1)
                )
            nc.vector.tensor_copy(out=bias_t[:], in_=bias_ps[:, 0:cols])

        def turn_whh_pairs(j, engines):
            for pair in range(2):
                whh_t_ps = cell_psum.tile([P, 2, 2, P], F32, tag="cell", name="whh_t_ps")
                for a in range(2):
                    for half in range(2):
                        nc.tensor.transpose(
                            whh_t_ps[:, half, a, :],
                            whh_sb[:, j, 2 * pair + a, :].bitcast(F32)[:, P * half : P * (half + 1)],
                            ident_f32[:],
                        )
                first = H * j + 2 * P * pair
                dst = whh_t[:, :, first : first + 2 * P]
                src = whh_t_ps[:].rearrange("w h a p -> w h (a p)")
                if engines[pair] == "v":
                    nc.vector.tensor_copy(out=dst, in_=src)
                else:
                    nc.scalar.copy(out=dst, in_=src)

        def turn_whh(j, engines):
            if j == GATE_I:
                return turn_whh_pairs(j, engines)
            for half in range(2):
                whh_t_ps = cell_psum.tile([P, 4, P], F32, tag="cell", name="whh_t_ps")
                for a in range(4):
                    nc.tensor.transpose(
                        whh_t_ps[:, a, :],
                        whh_sb[:, j, a, :].bitcast(F32)[:, P * half : P * (half + 1)],
                        ident_f32[:],
                    )
                dst = whh_t[:, half, H * j : H * (j + 1)].rearrange("w (p a) -> w p a", a=4)
                src = whh_t_ps[:].rearrange("w a p -> w p a")
                if engines[half] == "v":
                    nc.vector.tensor_copy(out=dst, in_=src)
                else:
                    nc.scalar.copy(out=dst, in_=src)

        const_banks = {}

        def make_const(j):
            multiply_h0(j)
            copy_const(j)

        def multiply_h0(j):
            const_ps = psum.tile([P, H], F32, tag="bank", name="const_ps")
            const_banks[j] = const_ps
            if j == GATE_O:
                for half in range(2):
                    for e in range(2):
                        nc.tensor.matmul(
                            out=const_ps[:],
                            lhsT=h0_rows[:, half, e, :],
                            rhs=whh_t[:, half, H * j : H * (j + 1)].bitcast(BF16).rearrange("w (n e) -> w n e", e=2)[:, :, e],
                            start=(half == 0 and e == 0),
                            stop=False,
                        )
                nc.tensor.matmul(out=const_ps[:], lhsT=ones[:], rhs=bias_rows_o[:], start=False, stop=True)
                return
            for blk in range(BLOCKS):
                cols = slice(H * j + P * blk, H * j + P * (blk + 1))
                for half in range(2):
                    for e in range(2):
                        nc.tensor.matmul(
                            out=const_ps[:, P * blk : P * (blk + 1)],
                            lhsT=whh_t[:, half, cols].bitcast(BF16).rearrange("w (n e) -> w n e", e=2)[:, :, e],
                            rhs=h0_rows[:, half, e, :],
                            start=(half == 0 and e == 0),
                            stop=(half == 1 and e == 1),
                        )

        def copy_const(j):
            const_ps = const_banks[j]
            if j == GATE_O:
                nc.vector.tensor_copy(out=const_o[:], in_=const_ps[:])
                return
            for blk in range(BLOCKS):
                place = BLOCKS * j + blk
                nc.vector.tensor_scalar(
                    out=const_t[:, j, blk, :],
                    in0=const_ps[:, P * blk : P * (blk + 1)],
                    scalar1=bias_t[:, place : place + 1],
                    scalar2=None,
                    op0=ALU.add,
                )

        fixed_ps = fixed_psum.tile([P, 2, H], BF16)
        c0_ps = fixed_ps[:, 0].rearrange("p (k b) -> p k b", k=BLOCKS)
        noise_ps = fixed_ps[:, 1]
        c0_t = keep.tile([P, G_BLOCKS, P], F32)
        times = [keep.tile([P, WIDE + G_COLS], F32, name="times%d" % m) for m in range(2)]

        def fix_in_psum():
            for blk in range(BLOCKS):
                nc.tensor.transpose(c0_ps[:, blk, :], c0_sb[:, P * blk : P * (blk + 1)], ident_bf16[:])
            nc.tensor.matmul(out=noise_ps, lhsT=ident_bf16[:], rhs=noise_sb[:], start=True, stop=True)
            nc.scalar.copy(out=c0_t[:], in_=c0_ps[:, 0:G_BLOCKS, :])
            for m in range(2):
                nc.gpsimd.tensor_scalar(
                    out=times[m][:, WIDE:].rearrange("p (k s b) -> p k s b", k=G_BLOCKS, s=PAIR),
                    in0=c0_t[:].unsqueeze(2).to_broadcast([P, G_BLOCKS, PAIR, P]),
                    scalar1=1.0,
                    scalar2=0.0,
                    op0=ALU.mult,
                    op1=ALU.add,
                )

        group_shape = [P, PAIR, H]
        noise_bc = noise_ps.unsqueeze(1).to_broadcast(group_shape)
        i_f, o_gate, products, cell, tanh_c, o_tanh_c, banks = {}, {}, {}, {}, {}, {}, {}

        def gate_columns(n, gate):
            if gate == GATE_O:
                return o_gate[n][:]
            if gate == GATE_G:
                return times[n % 2][:, 0:WIDE]
            return i_f[n][:, WIDE * gate : WIDE * (gate + 1)]

        def multiply(n, gate):
            first = PAIR * n
            for bank in range(2):
                if gate == GATE_O:
                    gate_ps = psum.tile([P, H], F32, tag="bank", name="gate_ps")
                    nc.tensor.matmul_mx(
                        out=gate_ps[:],
                        lhsT=x_codes[:, first + bank, :].bitcast(FP8X4),
                        lhsT_scale=x_scales[:, first + bank, :],
                        rhs=w_words[:, 2 * H * gate : 2 * H * (gate + 1)].bitcast(FP4X4),
                        rhs_scale=w_scale_plane[:, H * gate : H * (gate + 1)],
                        start=True,
                        stop=True,
                    )
                else:
                    gate_ps = psum.tile([P, 2, PAIR, P], F32, tag="bank", name="gate_ps")
                    for k in range(2):
                        col = H * gate + P * (2 * bank + k)
                        nc.tensor.matmul_mx(
                            out=gate_ps[:, k].rearrange("p s b -> p (s b)"),
                            lhsT=w_words[:, 2 * col : 2 * (col + P)].bitcast(FP4X4),
                            lhsT_scale=w_scale_plane[:, col : col + P],
                            rhs=x_codes[:, first : first + PAIR, :].rearrange("p s b -> p (s b)").bitcast(FP8X4),
                            rhs_scale=x_scales[:, first : first + PAIR, :].rearrange("p s b -> p (s b)"),
                            start=True,
                            stop=True,
                        )
                banks[n, gate, bank] = gate_ps

        def add_const(n, gate):
            for bank in range(2):
                half = gate_columns(n, gate)[:, H * bank : H * (bank + 1)]
                if gate == GATE_O:
                    nc.vector.tensor_tensor(out=half, in0=banks[n, gate, bank][:], in1=const_o[:], op=ALU.add)
                else:
                    nc.vector.tensor_tensor(
                        out=half.rearrange("p (k s b) -> p k s b", k=2, s=PAIR),
                        in0=banks[n, gate, bank][:],
                        in1=const_t[:, gate, 2 * bank : 2 * bank + 2, :].unsqueeze(2).to_broadcast([P, 2, PAIR, P]),
                        op=ALU.add,
                    )

        def activate(n, gate):
            columns = gate_columns(n, gate)
            nc.scalar.activation(out=columns, in_=columns, func=(ACT.Tanh if gate == GATE_G else ACT.Sigmoid))

        def start_group(n):
            i_f[n] = work.tile([P, 2 * WIDE], F32, bufs=3, name="i_f")
            o_gate[n] = work.tile([P, WIDE], F32, bufs=3, name="o_gate")
            products[n] = work.tile([P, 2, BLOCKS, PAIR, P], F32, bufs=2, name="products")

        def multiply_i_g_and_f_c0(n):
            if n in ALONE:
                nc.gpsimd.tensor_tensor(
                    out=products[n][:, 0].rearrange("p k s b -> p (k s b)"),
                    in0=i_f[n][:, 0:WIDE],
                    in1=times[n % 2][:, 0:WIDE],
                    op=ALU.mult,
                )
                return
            nc.gpsimd.tensor_tensor(
                out=products[n][:].rearrange("p h k s b -> p (h k s b)")[:, 0 : WIDE + G_COLS],
                in0=i_f[n][:, 0 : WIDE + G_COLS],
                in1=times[n % 2][:],
                op=ALU.mult,
            )

        def multiply_i_g_alone(n):
            nc.gpsimd.tensor_tensor(
                out=products[n][:, 0].rearrange("p k s b -> p (k s b)"),
                in0=i_f[n][:, 0:WIDE],
                in1=times[n % 2][:, 0:WIDE],
                op=ALU.mult,
            )

        def multiply_f_c0(n):
            skip = G_BLOCKS if n not in ALONE else 0
            count = BLOCKS - skip
            nc.vector.tensor_tensor(
                out=products[n][:, 1, skip:],
                in0=i_f[n][:, WIDE + skip * PAIR * P :].rearrange("p (k s b) -> p k s b", k=count, s=PAIR),
                in1=c0_ps[:, skip:, :].unsqueeze(2).to_broadcast([P, count, PAIR, P]),
                op=ALU.mult,
            )

        def sum_cell(n, s):
            c_ps = cell_psum.tile([P, BLOCKS, P], F32, tag="cell", name="c_ps")
            for k in range(2):
                for blk in range(BLOCKS):
                    nc.tensor.matmul(
                        out=c_ps[:, blk, :],
                        lhsT=products[n][:, k, blk, s, :],
                        rhs=ident_f32[:],
                        is_transpose=True,
                        start=(k == 0 and blk == 0),
                        stop=(k == 1 and blk == BLOCKS - 1),
                    )
            cell[n, s] = c_ps

        def tanh_cell(n, s):
            if s == 0:
                tanh_c[n] = work.tile(group_shape, F32, name="tanh_c")
            c_row = cell[n, s][:].rearrange("p k b -> p (k b)")
            nc.scalar.activation(out=tanh_c[n][:, s], in_=c_row, func=ACT.Tanh)
            if first_step(n) + s == STEPS - 1:
                c_last = keep.tile([P, H], F32)
                nc.scalar.copy(out=c_last[:], in_=c_row)
                nc.scalar.dma_start(out=out_state[1], in_=c_last[:])

        def pieces(n):
            if n < GROUPS - 1:
                return [slice(0, PAIR)]
            return [slice(s, s + 1) for s in range(PAIR)]

        def multiply_o(n):
            o_tanh_c[n] = work.tile(group_shape, F32, name="o_tanh_c")
            engine = nc.vector if n >= MO_V else nc.gpsimd
            for steps in pieces(n):
                engine.tensor_tensor(
                    out=o_tanh_c[n][:, steps],
                    in0=o_gate[n][:].rearrange("p (s m) -> p s m", s=PAIR)[:, steps],
                    in1=tanh_c[n][:, steps],
                    op=ALU.mult,
                )

        def store_h(n):
            h = work.tile(group_shape, F32, name="h")
            for steps in pieces(n):
                nc.vector.tensor_tensor(out=h[:, steps], in0=o_tanh_c[n][:, steps], in1=noise_bc[:, steps], op=ALU.add)
                first = first_step(n)
                nc.sync.dma_start(
                    out=out_h[first + steps.start : first + steps.stop].rearrange("t b m -> b t m"),
                    in_=h[:, steps],
                )
            if first_step(n) + PAIR == STEPS:
                nc.scalar.dma_start(out=out_state[0], in_=h[:, PAIR - 1, :])

        turn_h0()
        warm_tensor(2)
        turn_whh(GATE_I, "vs")
        turn_x(0, 0)
        copy_x(0, 0)
        turn_x(0, 1)
        copy_x(0, 1)
        turn_bias()
        quantise_x(0)
        make_const(GATE_I)
        turn_whh(GATE_G, "vs")
        start_group(0)
        multiply(0, GATE_I)
        add_const(0, GATE_I)
        make_const(GATE_G)
        turn_whh(GATE_F, "ss")
        multiply(0, GATE_G)
        activate(0, GATE_I)
        add_const(0, GATE_G)
        activate(0, GATE_G)
        make_const(GATE_F)
        turn_whh(GATE_O, "ss")
        fix_in_psum()
        multiply(0, GATE_F)
        add_const(0, GATE_F)
        activate(0, GATE_F)
        multiply_i_g_and_f_c0(0)
        make_const(GATE_O)
        multiply(0, GATE_O)
        add_const(0, GATE_O)
        activate(0, GATE_O)
        turn_x(1, 0)
        copy_x(1, 0)
        multiply_f_c0(0)

        for n in range(1, GROUPS + 2):
            here, before = n < GROUPS, 1 <= n <= GROUPS
            load, q = divmod(n + 2, 2)
            if n == GROUPS:
                warm_tensor(6)
            if load < LOADS:
                turn_x(load, q)
            if here:
                start_group(n)
                multiply(n, GATE_I)
                add_const(n, GATE_I)
            if load < LOADS:
                copy_x(load, q)
            if here:
                activate(n, GATE_I)
                multiply(n, GATE_G)
                add_const(n, GATE_G)
                activate(n, GATE_G)
                multiply(n, GATE_F)
                add_const(n, GATE_F)
                multiply(n, GATE_O)
                activate(n, GATE_F)
            if before:
                sum_cell(n - 1, 0)
                sum_cell(n - 1, 1)
                tanh_cell(n - 1, 0)
            if here:
                multiply_i_g_and_f_c0(n)
                add_const(n, GATE_O)
            if before:
                tanh_cell(n - 1, 1)
            if load < LOADS and q == 1:
                quantise_x(load)
            if n >= 2:
                store_h(n - 2)
            if here:
                multiply_f_c0(n)
                activate(n, GATE_O)
            if before:
                multiply_o(n - 1)
